import numpy as np
import ml_dtypes


def mxq(x, axis, fmt="e4m3"):
    dtype, down = {"e4m3": (ml_dtypes.float8_e4m3fn, 7), "e5m2": (ml_dtypes.float8_e5m2, 14)}[fmt]
    v = np.moveaxis(np.asarray(x, np.float32).astype(ml_dtypes.bfloat16).astype(np.float64), axis, -1)
    blocks = v.reshape(v.shape[:-1] + (-1, 32))
    amax = np.abs(blocks).max(-1, keepdims=True)
    byte = np.maximum(np.where(amax > 0, np.frexp(amax)[1] - 1 + 127, 0) - down, 1)
    scale = np.exp2(byte - 127.0)
    codes = (blocks / scale).astype(np.float32).astype(dtype).astype(np.float64)
    return np.moveaxis((codes * scale).reshape(v.shape), -1, axis)


WIDE = False


def mx_kscale(k):
    if not WIDE:
        return np.ones(k)
    levels = np.array([10, -10, 5, -5, 0])
    a = np.random.permutation(np.resize(levels, k // 512 * 4)).reshape(k // 512, 4)
    idx = np.arange(k)
    return np.exp2(a[idx // 512, idx % 128 // 32])


BF16 = ml_dtypes.bfloat16


def bf(x):
    return np.asarray(x, np.float32).astype(BF16)


def f64(x):
    return np.asarray(x).astype(np.float64)


N, CI, CO, H, W, KH, KW = 2, 128, 384, 18, 18, 3, 3
HO, WO = H - KH + 1, W - KW + 1
L = N * HO * WO


def setup_inputs():
    u = np.unique(mx_kscale(L))
    sn = u[(np.arange(N) * (len(u) - 1)) % len(u)][:, None, None, None]
    return {"input": bf(np.random.standard_normal((N, CI, H, W)) / sn),
            "grad_output": bf(np.random.standard_normal((N, CO, HO, WO)) / np.sqrt(L) * sn)}


def reference(input, grad_output):
    x = f64(input)
    gq = mxq(f64(grad_output).transpose(1, 0, 2, 3).reshape(CO, L), 1, "e4m3")
    taps = []
    for i in range(KH):
        for j in range(KW):
            patch = x[:, :, i:i + HO, j:j + WO].transpose(1, 0, 2, 3).reshape(CI, L)
            taps.append(gq @ mxq(patch, 1, "e4m3").T)
    return np.stack(taps, axis=-1).reshape(CO, CI, KH, KW)

@@ -1,0 +1,149 @@
+import concourse.mybir as mybir
+from concourse.masks import make_identity
+
+F32 = mybir.dt.float32
+BF16 = mybir.dt.bfloat16
+U32 = mybir.dt.uint32
+U8 = mybir.dt.uint8
+FP8X4 = mybir.dt.float8_e4m3fn_x4
+
+P = 128
+N_IMG, C_IN, C_OUT, H, W, KH, KW = 2, 128, 384, 18, 18, 3, 3
+HO, WO = H - KH + 1, W - KW + 1
+TAPS = KH * KW
+W_WORDS = W // 2
+WO_WORDS = WO // 2
+ROW_PAIRS = HO // 2
+ROW_SETS = KH + 1
+O_TILES = C_OUT // P
+BANK = 512
+CH_PER_BANK = BANK // TAPS
+PASS_WIDTHS = (128, 256, 512)
+
+FLOPS = 2 * C_OUT * C_IN * TAPS * N_IMG * HO * WO
+
+
+def tile_model_pa_s_kernel(tc, x, grad_output, out):
+    nc = tc.nc
+
+    groups = [(c0, min(CH_PER_BANK, C_IN - c0)) for c0 in range(0, C_IN, CH_PER_BANK)]
+    widths = [min(n for n in PASS_WIDTHS if n >= TAPS * cg) for (c0, cg) in groups]
+
+    with tc.tile_pool(name="keep", bufs=1) as keep, tc.tile_pool(
+        name="results", bufs=len(groups) * O_TILES
+    ) as results, tc.psum_pool(name="psum", bufs=8) as psum:
+
+        def copy(on_scalar, dst, src):
+            if on_scalar:
+                nc.scalar.copy(out=dst, in_=src)
+            else:
+                nc.vector.tensor_copy(out=dst, in_=src)
+
+        x_rows = x.rearrange("n c h w -> c n (h w)")
+        x_even = keep.tile([P, N_IMG, H * W], BF16)
+        nc.sync.dma_start(out=x_even[:], in_=x_rows)
+        x_odd = keep.tile([P, N_IMG, H * W], BF16)
+        nc.sync.dma_start(out=x_odd[:, :, 0 : H * W - 1], in_=x_rows[:, :, 1 : H * W])
+        g_in = []
+        for ot in range(O_TILES):
+            g_sb = keep.tile([P, N_IMG * HO * WO], BF16, name="g_sb%d" % ot)
+            nc.scalar.dma_start(
+                out=g_sb[:].rearrange("o (n k) -> o n k", n=N_IMG),
+                in_=grad_output[:, ot * P : (ot + 1) * P].rearrange("n o i j -> o n (i j)"),
+            )
+            g_in.append(g_sb)
+
+        ident = keep.tile([P, P], F32)
+        make_identity(nc, ident[:])
+
+        x_grouped, x_codes, x_scales = [], [], []
+        for grp, (c0, cg) in enumerate(groups):
+            grouped = keep.tile([P, 4 * widths[grp]], BF16, align_bytes=64, name="x_grouped%d" % grp)
+            nc.vector.memset(grouped[:, 4 * TAPS * cg :], 0.0)
+            x_grouped.append(grouped)
+            x_codes.append(keep.tile([P, widths[grp]], U32, align_bytes=64, name="x_codes%d" % grp))
+            x_scales.append(keep.tile([P, widths[grp]], U8, align_bytes=64, name="x_scales%d" % grp))
+        g_codes = keep.tile([P, C_OUT], U32, align_bytes=64)
+        g_scales = keep.tile([P, C_OUT], U8, align_bytes=64)
+
+        def prepare_windows(kw, on_scalar):
+            source = x_odd if kw % 2 else x_even
+            words = source[:].bitcast(F32).rearrange("c n (h w) -> c n h w", w=W_WORDS)
+            row_sets = keep.tile([P, ROW_SETS, P], F32, name="row_sets%d" % kw)
+            for a in range(ROW_SETS // 2):
+                nc.vector.tensor_copy(
+                    out=row_sets[:, 2 * a : 2 * a + 2, :].rearrange(
+                        "c b (n i w) -> c b n i w", n=N_IMG, i=ROW_PAIRS
+                    ),
+                    in_=words[:, :, 2 * a : 2 * a + HO, kw // 2 : kw // 2 + WO_WORDS].rearrange(
+                        "c n (i b) w -> c b n i w", b=2
+                    ),
+                )
+            x_t = psum.tile([P, ROW_SETS, P], F32, tag="bank", name="x_t%d" % kw)
+            for r in range(ROW_SETS):
+                nc.tensor.transpose(out=x_t[:, r, :], in_=row_sets[:, r, :], identity=ident[:])
+            for grp, (c0, cg) in enumerate(groups):
+                grouped_words = x_grouped[grp][:].bitcast(F32)
+                for kh in range(KH):
+                    tap = kh * KW + kw
+                    copy(
+                        on_scalar,
+                        grouped_words[:, 2 * tap * cg : 2 * (tap + 1) * cg].rearrange(
+                            "p (c u) -> p c u", u=2
+                        ),
+                        x_t[:, kh : kh + 2, c0 : c0 + cg].rearrange("p u c -> p c u"),
+                    )
+
+        def prepare_grad(ot):
+            row_sets = keep.tile([P, 2, P], F32, name="g_row_sets%d" % ot)
+            nc.scalar.copy(
+                out=row_sets[:].rearrange("o u (m w) -> o u m w", w=WO_WORDS),
+                in_=g_in[ot][:].bitcast(F32).rearrange("o (m u w) -> o u m w", u=2, w=WO_WORDS),
+            )
+            g_t = psum.tile([P, 2, P], F32, tag="bank", name="g_t%d" % ot)
+            for u in range(2):
+                nc.tensor.transpose(out=g_t[:, u, :], in_=row_sets[:, u, :], identity=ident[:])
+            grouped = keep.tile([P, 4 * P], BF16, align_bytes=64, name="g_grouped%d" % ot)
+            nc.scalar.copy(
+                out=grouped[:].bitcast(F32).rearrange("p (o u) -> p o u", u=2),
+                in_=g_t[:].rearrange("p u o -> p o u"),
+            )
+            o_cols = slice(ot * P, (ot + 1) * P)
+            nc.vector.quantize_mx(
+                out=g_codes[:, o_cols].bitcast(FP8X4), scales=g_scales[:, o_cols], in_=grouped[:]
+            )
+
+        prepare_windows(0, on_scalar=True)
+        prepare_windows(2, on_scalar=False)
+        for ot in range(O_TILES):
+            prepare_grad(ot)
+        prepare_windows(1, on_scalar=True)
+
+        for grp in range(len(groups)):
+            nc.vector.quantize_mx(
+                out=x_codes[grp][:].bitcast(FP8X4), scales=x_scales[grp][:], in_=x_grouped[grp][:]
+            )
+
+        for grp, (c0, cg) in enumerate(groups):
+            for ot in range(O_TILES):
+                o_cols = slice(ot * P, (ot + 1) * P)
+                acc = psum.tile([P, BANK], F32, tag="bank", name="acc")
+                nc.tensor.matmul_mx(
+                    out=acc[:, 0 : widths[grp]],
+                    lhsT=g_codes[:, o_cols].bitcast(FP8X4),
+                    lhsT_scale=g_scales[:, o_cols],
+                    rhs=x_codes[grp][:].bitcast(FP8X4),
+                    rhs_scale=x_scales[grp][:],
+                    start=True,
+                    stop=True,
+                )
+                res = results.tile([P, TAPS * CH_PER_BANK], F32, name="res")
+                copy(
+                    (grp * O_TILES + ot) % 2 == 1,
+                    res[:, 0 : TAPS * cg].rearrange("o (c t) -> o c t", t=TAPS),
+                    acc[:, 0 : TAPS * cg].rearrange("o (t c) -> o c t", t=TAPS),
+                )
+                nc.sync.dma_start(
+                    out=out[o_cols, c0 : c0 + cg].rearrange("o c kh kw -> o (c kh kw)"),
+                    in_=res[:, 0 : TAPS * cg],
+                )

@@ -19,6 +19,7 @@ O_TILES = C_OUT // P
 BANK = 512
 CH_PER_BANK = BANK // TAPS
 PASS_WIDTHS = (128, 256, 512)
+PSUM_BANKS = 8
 
 FLOPS = 2 * C_OUT * C_IN * TAPS * N_IMG * HO * WO
 
@@ -31,7 +32,7 @@ def tile_model_pa_s_kernel(tc, x, grad_output, out):
 
     with tc.tile_pool(name="keep", bufs=1) as keep, tc.tile_pool(
         name="results", bufs=len(groups) * O_TILES
-    ) as results, tc.psum_pool(name="psum", bufs=8) as psum:
+    ) as results, tc.psum_pool(name="psum", bufs=PSUM_BANKS - KW) as psum, tc.manual_schedule():
 
         def copy(on_scalar, dst, src):
             if on_scalar:
@@ -41,17 +42,20 @@ def tile_model_pa_s_kernel(tc, x, grad_output, out):
 
         x_rows = x.rearrange("n c h w -> c n (h w)")
         x_even = keep.tile([P, N_IMG, H * W], BF16)
-        nc.sync.dma_start(out=x_even[:], in_=x_rows)
         x_odd = keep.tile([P, N_IMG, H * W], BF16)
-        nc.sync.dma_start(out=x_odd[:, :, 0 : H * W - 1], in_=x_rows[:, :, 1 : H * W])
-        g_in = []
-        for ot in range(O_TILES):
-            g_sb = keep.tile([P, N_IMG * HO * WO], BF16, name="g_sb%d" % ot)
-            nc.scalar.dma_start(
-                out=g_sb[:].rearrange("o (n k) -> o n k", n=N_IMG),
+        g_in = [keep.tile([P, N_IMG * HO * WO], BF16, name="g_in%d" % ot) for ot in range(O_TILES)]
+
+        def load_grad(ot):
+            nc.sync.dma_start(
+                out=g_in[ot][:].rearrange("o (n k) -> o n k", n=N_IMG),
                 in_=grad_output[:, ot * P : (ot + 1) * P].rearrange("n o i j -> o n (i j)"),
             )
-            g_in.append(g_sb)
+
+        nc.sync.dma_start(out=x_even[:], in_=x_rows)
+        load_grad(0)
+        nc.sync.dma_start(out=x_odd[:, :, 0 : H * W - 1], in_=x_rows[:, :, 1 : H * W])
+        load_grad(1)
+        load_grad(2)
 
         ident = keep.tile([P, P], F32)
         make_identity(nc, ident[:])
@@ -63,87 +67,124 @@ def tile_model_pa_s_kernel(tc, x, grad_output, out):
             x_grouped.append(grouped)
             x_codes.append(keep.tile([P, widths[grp]], U32, align_bytes=64, name="x_codes%d" % grp))
             x_scales.append(keep.tile([P, widths[grp]], U8, align_bytes=64, name="x_scales%d" % grp))
+        g_grouped = [
+            keep.tile([P, 4 * P], BF16, align_bytes=64, name="g_grouped%d" % ot) for ot in range(O_TILES)
+        ]
         g_codes = keep.tile([P, C_OUT], U32, align_bytes=64)
         g_scales = keep.tile([P, C_OUT], U8, align_bytes=64)
 
-        def prepare_windows(kw, on_scalar):
+        x_row_sets = [keep.tile([P, ROW_SETS, P], F32, name="x_row_sets%d" % kw) for kw in range(KW)]
+        x_t = [
+            psum.tile([P, ROW_SETS, P], F32, name="x_t%d" % kw, tag="x_t%d" % kw, bufs=1)
+            for kw in range(KW)
+        ]
+
+        def gather_window_rows(kw):
             source = x_odd if kw % 2 else x_even
             words = source[:].bitcast(F32).rearrange("c n (h w) -> c n h w", w=W_WORDS)
-            row_sets = keep.tile([P, ROW_SETS, P], F32, name="row_sets%d" % kw)
             for a in range(ROW_SETS // 2):
                 nc.vector.tensor_copy(
-                    out=row_sets[:, 2 * a : 2 * a + 2, :].rearrange(
+                    out=x_row_sets[kw][:, 2 * a : 2 * a + 2, :].rearrange(
                         "c b (n i w) -> c b n i w", n=N_IMG, i=ROW_PAIRS
                     ),
                     in_=words[:, :, 2 * a : 2 * a + HO, kw // 2 : kw // 2 + WO_WORDS].rearrange(
                         "c n (i b) w -> c b n i w", b=2
                     ),
                 )
-            x_t = psum.tile([P, ROW_SETS, P], F32, tag="bank", name="x_t%d" % kw)
+
+        def transpose_window_rows(kw):
             for r in range(ROW_SETS):
-                nc.tensor.transpose(out=x_t[:, r, :], in_=row_sets[:, r, :], identity=ident[:])
-            for grp, (c0, cg) in enumerate(groups):
-                grouped_words = x_grouped[grp][:].bitcast(F32)
-                for kh in range(KH):
-                    tap = kh * KW + kw
-                    copy(
-                        on_scalar,
-                        grouped_words[:, 2 * tap * cg : 2 * (tap + 1) * cg].rearrange(
-                            "p (c u) -> p c u", u=2
-                        ),
-                        x_t[:, kh : kh + 2, c0 : c0 + cg].rearrange("p u c -> p c u"),
-                    )
+                nc.tensor.transpose(out=x_t[kw][:, r, :], in_=x_row_sets[kw][:, r, :], identity=ident[:])
 
-        def prepare_grad(ot):
-            row_sets = keep.tile([P, 2, P], F32, name="g_row_sets%d" % ot)
-            nc.scalar.copy(
-                out=row_sets[:].rearrange("o u (m w) -> o u m w", w=WO_WORDS),
-                in_=g_in[ot][:].bitcast(F32).rearrange("o (m u w) -> o u m w", u=2, w=WO_WORDS),
-            )
-            g_t = psum.tile([P, 2, P], F32, tag="bank", name="g_t%d" % ot)
-            for u in range(2):
-                nc.tensor.transpose(out=g_t[:, u, :], in_=row_sets[:, u, :], identity=ident[:])
-            grouped = keep.tile([P, 4 * P], BF16, align_bytes=64, name="g_grouped%d" % ot)
-            nc.scalar.copy(
-                out=grouped[:].bitcast(F32).rearrange("p (o u) -> p o u", u=2),
-                in_=g_t[:].rearrange("p u o -> p o u"),
-            )
-            o_cols = slice(ot * P, (ot + 1) * P)
-            nc.vector.quantize_mx(
-                out=g_codes[:, o_cols].bitcast(FP8X4), scales=g_scales[:, o_cols], in_=grouped[:]
-            )
+        def group_window_words(kw, grp):
+            c0, cg = groups[grp]
+            grouped_words = x_grouped[grp][:].bitcast(F32)
+            for kh in range(KH):
+                tap = kh * KW + kw
+                copy(
+                    kw != 2,
+                    grouped_words[:, 2 * tap * cg : 2 * (tap + 1) * cg].rearrange(
+                        "p (c u) -> p c u", u=2
+                    ),
+                    x_t[kw][:, kh : kh + 2, c0 : c0 + cg].rearrange("p u c -> p c u"),
+                )
 
-        prepare_windows(0, on_scalar=True)
-        prepare_windows(2, on_scalar=False)
-        for ot in range(O_TILES):
-            prepare_grad(ot)
-        prepare_windows(1, on_scalar=True)
-
-        for grp in range(len(groups)):
+        def quantise_windows(grp):
             nc.vector.quantize_mx(
                 out=x_codes[grp][:].bitcast(FP8X4), scales=x_scales[grp][:], in_=x_grouped[grp][:]
             )
 
-        for grp, (c0, cg) in enumerate(groups):
+        g_row_sets = [keep.tile([P, 2, P], F32, name="g_row_sets%d" % ot) for ot in range(O_TILES)]
+        g_t = {}
+
+        def split_grad_rows(ot):
+            nc.vector.tensor_copy(
+                out=g_row_sets[ot][:].rearrange("o u (m w) -> o u m w", w=WO_WORDS),
+                in_=g_in[ot][:].bitcast(F32).rearrange("o (m u w) -> o u m w", u=2, w=WO_WORDS),
+            )
+
+        def transpose_grad_rows(ot):
+            g_t[ot] = psum.tile([P, 2, P], F32, tag="bank", name="g_t%d" % ot)
+            for u in range(2):
+                nc.tensor.transpose(out=g_t[ot][:, u, :], in_=g_row_sets[ot][:, u, :], identity=ident[:])
+
+        def quantise_grad(ot):
+            nc.scalar.copy(
+                out=g_grouped[ot][:].bitcast(F32).rearrange("p (o u) -> p o u", u=2),
+                in_=g_t[ot][:].rearrange("p u o -> p o u"),
+            )
+            o_cols = slice(ot * P, (ot + 1) * P)
+            nc.vector.quantize_mx(
+                out=g_codes[:, o_cols].bitcast(FP8X4), scales=g_scales[:, o_cols], in_=g_grouped[ot][:]
+            )
+
+        def multiply_and_store(grp, ot):
+            c0, cg = groups[grp]
+            o_cols = slice(ot * P, (ot + 1) * P)
+            acc = psum.tile([P, BANK], F32, tag="bank", name="acc")
+            nc.tensor.matmul_mx(
+                out=acc[:, 0 : widths[grp]],
+                lhsT=g_codes[:, o_cols].bitcast(FP8X4),
+                lhsT_scale=g_scales[:, o_cols],
+                rhs=x_codes[grp][:].bitcast(FP8X4),
+                rhs_scale=x_scales[grp][:],
+                start=True,
+                stop=True,
+            )
+            res = results.tile([P, TAPS * CH_PER_BANK], F32, name="res")
+            copy(
+                (grp * O_TILES + ot) % 2 == 0,
+                res[:, 0 : TAPS * cg].rearrange("o (c t) -> o c t", t=TAPS),
+                acc[:, 0 : TAPS * cg].rearrange("o (t c) -> o c t", t=TAPS),
+            )
+            nc.sync.dma_start(
+                out=out[o_cols, c0 : c0 + cg].rearrange("o c kh kw -> o (c kh kw)"),
+                in_=res[:, 0 : TAPS * cg],
+            )
+
+        gather_window_rows(0)
+        transpose_window_rows(0)
+        gather_window_rows(2)
+        transpose_window_rows(2)
+        split_grad_rows(0)
+        transpose_grad_rows(0)
+        gather_window_rows(1)
+        transpose_window_rows(1)
+        for ot in range(1, O_TILES):
+            split_grad_rows(ot)
+            transpose_grad_rows(ot)
+        for grp in range(len(groups)):
+            group_window_words(0, grp)
+        for grp in range(len(groups)):
+            group_window_words(2, grp)
+        quantise_grad(0)
+        group_window_words(1, 0)
+        quantise_windows(0)
+        for ot in range(1, O_TILES):
+            quantise_grad(ot)
+        for grp in range(1, len(groups)):
+            group_window_words(1, grp)
+            quantise_windows(grp)
+        for grp in range(len(groups)):
             for ot in range(O_TILES):
-                o_cols = slice(ot * P, (ot + 1) * P)
-                acc = psum.tile([P, BANK], F32, tag="bank", name="acc")
-                nc.tensor.matmul_mx(
-                    out=acc[:, 0 : widths[grp]],
-                    lhsT=g_codes[:, o_cols].bitcast(FP8X4),
-                    lhsT_scale=g_scales[:, o_cols],
-                    rhs=x_codes[grp][:].bitcast(FP8X4),
-                    rhs_scale=x_scales[grp][:],
-                    start=True,
-                    stop=True,
-                )
-                res = results.tile([P, TAPS * CH_PER_BANK], F32, name="res")
-                copy(
-                    (grp * O_TILES + ot) % 2 == 1,
-                    res[:, 0 : TAPS * cg].rearrange("o (c t) -> o c t", t=TAPS),
-                    acc[:, 0 : TAPS * cg].rearrange("o (t c) -> o c t", t=TAPS),
-                )
-                nc.sync.dma_start(
-                    out=out[o_cols, c0 : c0 + cg].rearrange("o c kh kw -> o (c kh kw)"),
-                    in_=res[:, 0 : TAPS * cg],
-                )
+                multiply_and_store(grp, ot)

@@ -20,6 +20,8 @@ BANK = 512
 CH_PER_BANK = BANK // TAPS
 PASS_WIDTHS = (128, 256, 512)
 PSUM_BANKS = 8
+IDLE_MATMULS_HEAD = 5
+IDLE_MATMULS_MID = 3
 
 FLOPS = 2 * C_OUT * C_IN * TAPS * N_IMG * HO * WO
 
@@ -39,6 +41,14 @@ def tile_model_pa_s_kernel(tc, x, grad_output, out):
                 nc.scalar.copy(out=dst, in_=src)
             else:
                 nc.vector.tensor_copy(out=dst, in_=src)
+
+        zeros = keep.tile([P, P], F32)
+        nc.vector.memset(zeros[:], 0.0)
+
+        def multiply_zeros(matmuls):
+            idle_acc = psum.tile([P, P], F32, tag="bank", name="idle_acc")
+            for i in range(matmuls):
+                nc.tensor.matmul(out=idle_acc[:], lhsT=zeros[:], rhs=zeros[:], start=True, stop=True)
 
         x_rows = x.rearrange("n c h w -> c n (h w)")
         x_even = keep.tile([P, N_IMG, H * W], BF16)
@@ -162,6 +172,7 @@ def tile_model_pa_s_kernel(tc, x, grad_output, out):
                 in_=res[:, 0 : TAPS * cg],
             )
 
+        multiply_zeros(IDLE_MATMULS_HEAD)
         gather_window_rows(0)
         transpose_window_rows(0)
         gather_window_rows(2)
@@ -173,6 +184,7 @@ def tile_model_pa_s_kernel(tc, x, grad_output, out):
         for ot in range(1, O_TILES):
             split_grad_rows(ot)
             transpose_grad_rows(ot)
+        multiply_zeros(IDLE_MATMULS_MID)
         for grp in range(len(groups)):
             group_window_words(0, grp)
         for grp in range(len(groups)):

@@ -20,6 +20,7 @@ BANK = 512
 CH_PER_BANK = BANK // TAPS
 PASS_WIDTHS = (128, 256, 512)
 PSUM_BANKS = 8
+SHIFT_ORDER = (0, 2, 1)
 IDLE_MATMULS_HEAD = 5
 IDLE_MATMULS_MID = 3
 
@@ -62,10 +63,9 @@ def tile_model_pa_s_kernel(tc, x, grad_output, out):
             )
 
         nc.sync.dma_start(out=x_even[:], in_=x_rows)
-        load_grad(0)
         nc.sync.dma_start(out=x_odd[:, :, 0 : H * W - 1], in_=x_rows[:, :, 1 : H * W])
-        load_grad(1)
-        load_grad(2)
+        for ot in range(O_TILES):
+            load_grad(ot)
 
         ident = keep.tile([P, P], F32)
         make_identity(nc, ident[:])
@@ -92,14 +92,11 @@ def tile_model_pa_s_kernel(tc, x, grad_output, out):
         def gather_window_rows(kw):
             source = x_odd if kw % 2 else x_even
             words = source[:].bitcast(F32).rearrange("c n (h w) -> c n h w", w=W_WORDS)
-            for a in range(ROW_SETS // 2):
-                nc.vector.tensor_copy(
-                    out=x_row_sets[kw][:, 2 * a : 2 * a + 2, :].rearrange(
-                        "c b (n i w) -> c b n i w", n=N_IMG, i=ROW_PAIRS
-                    ),
-                    in_=words[:, :, 2 * a : 2 * a + HO, kw // 2 : kw // 2 + WO_WORDS].rearrange(
-                        "c n (i b) w -> c b n i w", b=2
-                    ),
+            for r in range(ROW_SETS):
+                copy(
+                    kw == 2,
+                    x_row_sets[kw][:, r, :].rearrange("c (n i w) -> c n i w", n=N_IMG, i=ROW_PAIRS),
+                    words[:, :, r : r + HO - 1 : 2, kw // 2 : kw // 2 + WO_WORDS],
                 )
 
         def transpose_window_rows(kw):
@@ -112,7 +109,7 @@ def tile_model_pa_s_kernel(tc, x, grad_output, out):
             for kh in range(KH):
                 tap = kh * KW + kw
                 copy(
-                    kw != 2,
+                    kw != 1,
                     grouped_words[:, 2 * tap * cg : 2 * (tap + 1) * cg].rearrange(
                         "p (c u) -> p c u", u=2
                     ),
@@ -128,9 +125,10 @@ def tile_model_pa_s_kernel(tc, x, grad_output, out):
         g_t = {}
 
         def split_grad_rows(ot):
-            nc.vector.tensor_copy(
-                out=g_row_sets[ot][:].rearrange("o u (m w) -> o u m w", w=WO_WORDS),
-                in_=g_in[ot][:].bitcast(F32).rearrange("o (m u w) -> o u m w", u=2, w=WO_WORDS),
+            copy(
+                ot == 0,
+                g_row_sets[ot][:].rearrange("o u (m w) -> o u m w", w=WO_WORDS),
+                g_in[ot][:].bitcast(F32).rearrange("o (m u w) -> o u m w", u=2, w=WO_WORDS),
             )
 
         def transpose_grad_rows(ot):
@@ -172,31 +170,24 @@ def tile_model_pa_s_kernel(tc, x, grad_output, out):
                 in_=res[:, 0 : TAPS * cg],
             )
 
+        def prepare_windows(grp):
+            for kw in SHIFT_ORDER:
+                group_window_words(kw, grp)
+            quantise_windows(grp)
+
         multiply_zeros(IDLE_MATMULS_HEAD)
-        gather_window_rows(0)
-        transpose_window_rows(0)
-        gather_window_rows(2)
-        transpose_window_rows(2)
-        split_grad_rows(0)
-        transpose_grad_rows(0)
-        gather_window_rows(1)
-        transpose_window_rows(1)
-        for ot in range(1, O_TILES):
+        for kw in SHIFT_ORDER:
+            gather_window_rows(kw)
+            transpose_window_rows(kw)
+        for ot in range(O_TILES):
             split_grad_rows(ot)
             transpose_grad_rows(ot)
         multiply_zeros(IDLE_MATMULS_MID)
-        for grp in range(len(groups)):
-            group_window_words(0, grp)
-        for grp in range(len(groups)):
-            group_window_words(2, grp)
-        quantise_grad(0)
-        group_window_words(1, 0)
-        quantise_windows(0)
-        for ot in range(1, O_TILES):
+        prepare_windows(0)
+        for ot in range(O_TILES):
             quantise_grad(ot)
-        for grp in range(1, len(groups)):
-            group_window_words(1, grp)
-            quantise_windows(grp)
         for grp in range(len(groups)):
+            if grp + 1 < len(groups):
+                prepare_windows(grp + 1)
             for ot in range(O_TILES):
                 multiply_and_store(grp, ot)

@@ -20,8 +20,7 @@ BANK = 512
 CH_PER_BANK = BANK // TAPS
 PASS_WIDTHS = (128, 256, 512)
 PSUM_BANKS = 8
-SHIFT_ORDER = (0, 2, 1)
-IDLE_MATMULS_HEAD = 5
+IDLE_MATMULS_HEAD = 4
 IDLE_MATMULS_MID = 3
 
 FLOPS = 2 * C_OUT * C_IN * TAPS * N_IMG * HO * WO
@@ -63,9 +62,10 @@ def tile_model_pa_s_kernel(tc, x, grad_output, out):
             )
 
         nc.sync.dma_start(out=x_even[:], in_=x_rows)
+        load_grad(0)
         nc.sync.dma_start(out=x_odd[:, :, 0 : H * W - 1], in_=x_rows[:, :, 1 : H * W])
-        for ot in range(O_TILES):
-            load_grad(ot)
+        load_grad(1)
+        load_grad(2)
 
         ident = keep.tile([P, P], F32)
         make_identity(nc, ident[:])
@@ -92,11 +92,14 @@ def tile_model_pa_s_kernel(tc, x, grad_output, out):
         def gather_window_rows(kw):
             source = x_odd if kw % 2 else x_even
             words = source[:].bitcast(F32).rearrange("c n (h w) -> c n h w", w=W_WORDS)
-            for r in range(ROW_SETS):
-                copy(
-                    kw == 2,
-                    x_row_sets[kw][:, r, :].rearrange("c (n i w) -> c n i w", n=N_IMG, i=ROW_PAIRS),
-                    words[:, :, r : r + HO - 1 : 2, kw // 2 : kw // 2 + WO_WORDS],
+            for a in range(ROW_SETS // 2):
+                nc.vector.tensor_copy(
+                    out=x_row_sets[kw][:, 2 * a : 2 * a + 2, :].rearrange(
+                        "c b (n i w) -> c b n i w", n=N_IMG, i=ROW_PAIRS
+                    ),
+                    in_=words[:, :, 2 * a : 2 * a + HO, kw // 2 : kw // 2 + WO_WORDS].rearrange(
+                        "c n (i b) w -> c b n i w", b=2
+                    ),
                 )
 
         def transpose_window_rows(kw):
@@ -109,7 +112,7 @@ def tile_model_pa_s_kernel(tc, x, grad_output, out):
             for kh in range(KH):
                 tap = kh * KW + kw
                 copy(
-                    kw != 1,
+                    kw != 2,
                     grouped_words[:, 2 * tap * cg : 2 * (tap + 1) * cg].rearrange(
                         "p (c u) -> p c u", u=2
                     ),
@@ -170,24 +173,31 @@ def tile_model_pa_s_kernel(tc, x, grad_output, out):
                 in_=res[:, 0 : TAPS * cg],
             )
 
-        def prepare_windows(grp):
-            for kw in SHIFT_ORDER:
-                group_window_words(kw, grp)
-            quantise_windows(grp)
-
         multiply_zeros(IDLE_MATMULS_HEAD)
-        for kw in SHIFT_ORDER:
-            gather_window_rows(kw)
-            transpose_window_rows(kw)
-        for ot in range(O_TILES):
+        gather_window_rows(0)
+        transpose_window_rows(0)
+        gather_window_rows(2)
+        transpose_window_rows(2)
+        split_grad_rows(0)
+        transpose_grad_rows(0)
+        gather_window_rows(1)
+        transpose_window_rows(1)
+        for ot in range(1, O_TILES):
             split_grad_rows(ot)
             transpose_grad_rows(ot)
         multiply_zeros(IDLE_MATMULS_MID)
-        prepare_windows(0)
-        for ot in range(O_TILES):
-            quantise_grad(ot)
         for grp in range(len(groups)):
-            if grp + 1 < len(groups):
-                prepare_windows(grp + 1)
+            group_window_words(0, grp)
+        for grp in range(len(groups)):
+            group_window_words(2, grp)
+        quantise_grad(0)
+        group_window_words(1, 0)
+        quantise_windows(0)
+        for ot in range(1, O_TILES):
+            quantise_grad(ot)
+        for grp in range(1, len(groups)):
+            group_window_words(1, grp)
+            quantise_windows(grp)
+        for grp in range(len(groups)):
             for ot in range(O_TILES):
                 multiply_and_store(grp, ot)

@@ -83,7 +83,10 @@ def tile_model_pa_s_kernel(tc, x, grad_output, out):
         g_codes = keep.tile([P, C_OUT], U32, align_bytes=64)
         g_scales = keep.tile([P, C_OUT], U8, align_bytes=64)
 
-        x_row_sets = [keep.tile([P, ROW_SETS, P], F32, name="x_row_sets%d" % kw) for kw in range(KW)]
+        x_rows_by_parity = [
+            keep.tile([P, 2, H // 2, N_IMG, WO_WORDS], F32, name="x_rows_by_parity%d" % kw)
+            for kw in range(KW)
+        ]
         x_t = [
             psum.tile([P, ROW_SETS, P], F32, name="x_t%d" % kw, tag="x_t%d" % kw, bufs=1)
             for kw in range(KW)
@@ -92,32 +95,33 @@ def tile_model_pa_s_kernel(tc, x, grad_output, out):
         def gather_window_rows(kw):
             source = x_odd if kw % 2 else x_even
             words = source[:].bitcast(F32).rearrange("c n (h w) -> c n h w", w=W_WORDS)
-            for a in range(ROW_SETS // 2):
-                nc.vector.tensor_copy(
-                    out=x_row_sets[kw][:, 2 * a : 2 * a + 2, :].rearrange(
-                        "c b (n i w) -> c b n i w", n=N_IMG, i=ROW_PAIRS
-                    ),
-                    in_=words[:, :, 2 * a : 2 * a + HO, kw // 2 : kw // 2 + WO_WORDS].rearrange(
-                        "c n (i b) w -> c b n i w", b=2
-                    ),
-                )
+            nc.vector.tensor_copy(
+                out=x_rows_by_parity[kw][:],
+                in_=words[:, :, :, kw // 2 : kw // 2 + WO_WORDS].rearrange("c n (m b) w -> c b m n w", b=2),
+            )
 
         def transpose_window_rows(kw):
             for r in range(ROW_SETS):
-                nc.tensor.transpose(out=x_t[kw][:, r, :], in_=x_row_sets[kw][:, r, :], identity=ident[:])
+                row_set = x_rows_by_parity[kw][:, r % 2, r // 2 : r // 2 + ROW_PAIRS, :, :]
+                nc.tensor.transpose(
+                    out=x_t[kw][:, r, :], in_=row_set.rearrange("c m n w -> c (m n w)"), identity=ident[:]
+                )
 
         def group_window_words(kw, grp):
             c0, cg = groups[grp]
-            grouped_words = x_grouped[grp][:].bitcast(F32)
-            for kh in range(KH):
-                tap = kh * KW + kw
-                copy(
-                    kw != 2,
-                    grouped_words[:, 2 * tap * cg : 2 * (tap + 1) * cg].rearrange(
-                        "p (c u) -> p c u", u=2
-                    ),
-                    x_t[kw][:, kh : kh + 2, c0 : c0 + cg].rearrange("p u c -> p c u"),
-                )
+            grouped_words = x_grouped[grp][:].bitcast(F32)[:, 0 : 2 * TAPS * cg].rearrange(
+                "p (kh kw c u) -> p kh kw c u", kh=KH, kw=KW, u=2
+            )
+            copy(
+                kw != 2,
+                grouped_words[:, 0:KH:2, kw, :, :],
+                x_t[kw][:, :, c0 : c0 + cg].rearrange("p (a u) c -> p a c u", u=2),
+            )
+            copy(
+                kw != 2,
+                grouped_words[:, 1, kw, :, :],
+                x_t[kw][:, 1:3, c0 : c0 + cg].rearrange("p u c -> p c u"),
+            )
 
         def quantise_windows(grp):
             nc.vector.quantize_mx(
@@ -130,8 +134,8 @@ def tile_model_pa_s_kernel(tc, x, grad_output, out):
         def split_grad_rows(ot):
             copy(
                 ot == 0,
-                g_row_sets[ot][:].rearrange("o u (m w) -> o u m w", w=WO_WORDS),
-                g_in[ot][:].bitcast(F32).rearrange("o (m u w) -> o u m w", u=2, w=WO_WORDS),
+                g_row_sets[ot][:].rearrange("o u (m n w) -> o u m n w", n=N_IMG, w=WO_WORDS),
+                g_in[ot][:].bitcast(F32).rearrange("o (n m u w) -> o u m n w", n=N_IMG, u=2, w=WO_WORDS),
             )
 
         def transpose_grad_rows(ot):

@@ -33,7 +33,7 @@ def tile_model_pa_s_kernel(tc, x, grad_output, out):
     widths = [min(n for n in PASS_WIDTHS if n >= TAPS * cg) for (c0, cg) in groups]
 
     with tc.tile_pool(name="keep", bufs=1) as keep, tc.tile_pool(
-        name="results", bufs=len(groups) * O_TILES
+        name="results", bufs=2 * O_TILES
     ) as results, tc.psum_pool(name="psum", bufs=PSUM_BANKS - KW) as psum, tc.manual_schedule():
 
         def copy(on_scalar, dst, src):
@@ -153,6 +153,9 @@ def tile_model_pa_s_kernel(tc, x, grad_output, out):
                 out=g_codes[:, o_cols].bitcast(FP8X4), scales=g_scales[:, o_cols], in_=g_grouped[ot][:]
             )
 
+        res_tiles = {}
+        turn = [0]
+
         def multiply_and_store(grp, ot):
             c0, cg = groups[grp]
             o_cols = slice(ot * P, (ot + 1) * P)
@@ -166,16 +169,21 @@ def tile_model_pa_s_kernel(tc, x, grad_output, out):
                 start=True,
                 stop=True,
             )
-            res = results.tile([P, TAPS * CH_PER_BANK], F32, name="res")
+            first_c = groups[min(grp, 1)][0]
+            if grp <= 1:
+                res_tiles[ot] = results.tile([P, TAPS * (C_IN - CH_PER_BANK)], F32, name="res")
+            res = res_tiles[ot]
+            turn[0] += 1
             copy(
-                (grp * O_TILES + ot) % 2 == 0,
-                res[:, 0 : TAPS * cg].rearrange("o (c t) -> o c t", t=TAPS),
+                turn[0] % 2 == 1,
+                res[:, TAPS * (c0 - first_c) : TAPS * (c0 + cg - first_c)].rearrange("o (c t) -> o c t", t=TAPS),
                 acc[:, 0 : TAPS * cg].rearrange("o (t c) -> o c t", t=TAPS),
             )
-            nc.sync.dma_start(
-                out=out[o_cols, c0 : c0 + cg].rearrange("o c kh kw -> o (c kh kw)"),
-                in_=res[:, 0 : TAPS * cg],
-            )
+            if grp == 0 or grp == len(groups) - 1:
+                nc.sync.dma_start(
+                    out=out[o_cols, first_c : c0 + cg].rearrange("o c kh kw -> o (c kh kw)"),
+                    in_=res[:, 0 : TAPS * (c0 + cg - first_c)],
+                )
 
         multiply_zeros(IDLE_MATMULS_HEAD)
         gather_window_rows(0)
@@ -202,6 +210,8 @@ def tile_model_pa_s_kernel(tc, x, grad_output, out):
         for grp in range(1, len(groups)):
             group_window_words(1, grp)
             quantise_windows(grp)
-        for grp in range(len(groups)):
-            for ot in range(O_TILES):
+        for ot in range(O_TILES):
+            multiply_and_store(0, ot)
+        for ot in range(O_TILES):
+            for grp in range(1, len(groups)):
                 multiply_and_store(grp, ot)

@@ -52,7 +52,6 @@ def tile_model_pa_s_kernel(tc, x, grad_output, out):
 
         x_rows = x.rearrange("n c h w -> c n (h w)")
         x_even = keep.tile([P, N_IMG, H * W], BF16)
-        x_odd = keep.tile([P, N_IMG, H * W], BF16)
         g_in = [keep.tile([P, N_IMG * HO * WO], BF16, name="g_in%d" % ot) for ot in range(O_TILES)]
 
         def load_grad(ot):
@@ -63,7 +62,6 @@ def tile_model_pa_s_kernel(tc, x, grad_output, out):
 
         nc.sync.dma_start(out=x_even[:], in_=x_rows)
         load_grad(0)
-        nc.sync.dma_start(out=x_odd[:, :, 0 : H * W - 1], in_=x_rows[:, :, 1 : H * W])
         load_grad(1)
         load_grad(2)
 
@@ -93,8 +91,15 @@ def tile_model_pa_s_kernel(tc, x, grad_output, out):
         ]
 
         def gather_window_rows(kw):
-            source = x_odd if kw % 2 else x_even
-            words = source[:].bitcast(F32).rearrange("c n (h w) -> c n h w", w=W_WORDS)
+            if kw % 2:
+                nc.scalar.copy(
+                    out=x_rows_by_parity[kw][:].bitcast(BF16),
+                    in_=x_even[:].rearrange("c n (h w) -> c n h w", w=W)[:, :, :, kw : kw + WO].rearrange(
+                        "c n (m b) w -> c b m n w", b=2
+                    ),
+                )
+                return
+            words = x_even[:].bitcast(F32).rearrange("c n (h w) -> c n h w", w=W_WORDS)
             nc.vector.tensor_copy(
                 out=x_rows_by_parity[kw][:],
                 in_=words[:, :, :, kw // 2 : kw // 2 + WO_WORDS].rearrange("c n (m b) w -> c b m n w", b=2),
@@ -187,12 +192,12 @@ def tile_model_pa_s_kernel(tc, x, grad_output, out):
 
         multiply_zeros(IDLE_MATMULS_HEAD)
         gather_window_rows(0)
+        gather_window_rows(1)
         transpose_window_rows(0)
         gather_window_rows(2)
         transpose_window_rows(2)
         split_grad_rows(0)
         transpose_grad_rows(0)
-        gather_window_rows(1)
         transpose_window_rows(1)
         for ot in range(1, O_TILES):
             split_grad_rows(ot)

@@ -21,7 +21,7 @@ CH_PER_BANK = BANK // TAPS
 PASS_WIDTHS = (128, 256, 512)
 PSUM_BANKS = 8
 IDLE_MATMULS_HEAD = 4
-IDLE_MATMULS_MID = 3
+IDLE_MATMULS_MID = 2
 
 FLOPS = 2 * C_OUT * C_IN * TAPS * N_IMG * HO * WO
 
@@ -112,25 +112,28 @@ def tile_model_pa_s_kernel(tc, x, grad_output, out):
                     out=x_t[kw][:, r, :], in_=row_set.rearrange("c m n w -> c (m n w)"), identity=ident[:]
                 )
 
-        def group_window_words(kw, grp):
+        def group_window_words(kw, grp, on_scalar):
             c0, cg = groups[grp]
             grouped_words = x_grouped[grp][:].bitcast(F32)[:, 0 : 2 * TAPS * cg].rearrange(
-                "p (kh kw c u) -> p kh kw c u", kh=KH, kw=KW, u=2
+                "p (kw kh c u) -> p kw kh c u", kh=KH, kw=KW, u=2
             )
             copy(
-                kw != 2,
-                grouped_words[:, 0:KH:2, kw, :, :],
+                on_scalar,
+                grouped_words[:, kw, 0:KH:2, :, :],
                 x_t[kw][:, :, c0 : c0 + cg].rearrange("p (a u) c -> p a c u", u=2),
             )
             copy(
-                kw != 2,
-                grouped_words[:, 1, kw, :, :],
+                on_scalar,
+                grouped_words[:, kw, 1, :, :],
                 x_t[kw][:, 1:3, c0 : c0 + cg].rearrange("p u c -> p c u"),
             )
 
-        def quantise_windows(grp):
+        def quantise_windows(grp, lo=0, hi=None):
+            hi = widths[grp] if hi is None else hi
             nc.vector.quantize_mx(
-                out=x_codes[grp][:].bitcast(FP8X4), scales=x_scales[grp][:], in_=x_grouped[grp][:]
+                out=x_codes[grp][:, lo:hi].bitcast(FP8X4),
+                scales=x_scales[grp][:, lo:hi],
+                in_=x_grouped[grp][:, 4 * lo : 4 * hi],
             )
 
         g_row_sets = [keep.tile([P, 2, P], F32, name="g_row_sets%d" % ot) for ot in range(O_TILES)]
@@ -148,75 +151,105 @@ def tile_model_pa_s_kernel(tc, x, grad_output, out):
             for u in range(2):
                 nc.tensor.transpose(out=g_t[ot][:, u, :], in_=g_row_sets[ot][:, u, :], identity=ident[:])
 
-        def quantise_grad(ot):
+        def group_grad_words(ot):
             nc.scalar.copy(
                 out=g_grouped[ot][:].bitcast(F32).rearrange("p (o u) -> p o u", u=2),
                 in_=g_t[ot][:].rearrange("p u o -> p o u"),
             )
+
+        def quantise_grad(ot):
             o_cols = slice(ot * P, (ot + 1) * P)
             nc.vector.quantize_mx(
                 out=g_codes[:, o_cols].bitcast(FP8X4), scales=g_scales[:, o_cols], in_=g_grouped[ot][:]
             )
 
+        accs = {}
         res_tiles = {}
-        turn = [0]
 
-        def multiply_and_store(grp, ot):
-            c0, cg = groups[grp]
+        def multiply(grp, ot, lo=0, hi=None):
+            hi = widths[grp] if hi is None else hi
             o_cols = slice(ot * P, (ot + 1) * P)
-            acc = psum.tile([P, BANK], F32, tag="bank", name="acc")
+            if lo == 0:
+                accs[(grp, ot)] = psum.tile([P, BANK], F32, tag="bank", name="acc")
             nc.tensor.matmul_mx(
-                out=acc[:, 0 : widths[grp]],
+                out=accs[(grp, ot)][:, lo:hi],
                 lhsT=g_codes[:, o_cols].bitcast(FP8X4),
                 lhsT_scale=g_scales[:, o_cols],
-                rhs=x_codes[grp][:].bitcast(FP8X4),
-                rhs_scale=x_scales[grp][:],
+                rhs=x_codes[grp][:, lo:hi].bitcast(FP8X4),
+                rhs_scale=x_scales[grp][:, lo:hi],
                 start=True,
                 stop=True,
             )
+
+        def copy_out(grp, ot, on_scalar):
+            c0, cg = groups[grp]
             first_c = groups[min(grp, 1)][0]
             if grp <= 1:
                 res_tiles[ot] = results.tile([P, TAPS * (C_IN - CH_PER_BANK)], F32, name="res")
-            res = res_tiles[ot]
-            turn[0] += 1
             copy(
-                turn[0] % 2 == 1,
-                res[:, TAPS * (c0 - first_c) : TAPS * (c0 + cg - first_c)].rearrange("o (c t) -> o c t", t=TAPS),
-                acc[:, 0 : TAPS * cg].rearrange("o (t c) -> o c t", t=TAPS),
+                on_scalar,
+                res_tiles[ot][:, TAPS * (c0 - first_c) : TAPS * (c0 + cg - first_c)].rearrange(
+                    "o (c kh kw) -> o c kh kw", kh=KH, kw=KW
+                ),
+                accs[(grp, ot)][:, 0 : TAPS * cg].rearrange("o (kw kh c) -> o c kh kw", kh=KH, kw=KW),
             )
-            if grp == 0 or grp == len(groups) - 1:
-                nc.sync.dma_start(
-                    out=out[o_cols, first_c : c0 + cg].rearrange("o c kh kw -> o (c kh kw)"),
-                    in_=res[:, 0 : TAPS * (c0 + cg - first_c)],
-                )
 
+        def store(first_grp, last_grp, ot):
+            first_c = groups[first_grp][0]
+            end_c = groups[last_grp][0] + groups[last_grp][1]
+            nc.sync.dma_start(
+                out=out[ot * P : (ot + 1) * P, first_c:end_c].rearrange("o c kh kw -> o (c kh kw)"),
+                in_=res_tiles[ot][:, 0 : TAPS * (end_c - first_c)],
+            )
+
+        SC, VE = True, False
+        half = widths[0] // 2
         multiply_zeros(IDLE_MATMULS_HEAD)
         gather_window_rows(0)
         gather_window_rows(1)
         transpose_window_rows(0)
         gather_window_rows(2)
-        transpose_window_rows(2)
+        transpose_window_rows(1)
         split_grad_rows(0)
         transpose_grad_rows(0)
-        transpose_window_rows(1)
-        for ot in range(1, O_TILES):
-            split_grad_rows(ot)
-            transpose_grad_rows(ot)
+        transpose_window_rows(2)
+        split_grad_rows(1)
+        transpose_grad_rows(1)
+        group_window_words(0, 0, SC)
+        group_window_words(1, 0, VE)
+        split_grad_rows(2)
+        transpose_grad_rows(2)
         multiply_zeros(IDLE_MATMULS_MID)
-        for grp in range(len(groups)):
-            group_window_words(0, grp)
-        for grp in range(len(groups)):
-            group_window_words(2, grp)
+        group_grad_words(0)
         quantise_grad(0)
-        group_window_words(1, 0)
-        quantise_windows(0)
-        for ot in range(1, O_TILES):
-            quantise_grad(ot)
-        for grp in range(1, len(groups)):
-            group_window_words(1, grp)
-            quantise_windows(grp)
+        quantise_windows(0, 0, half)
+        group_window_words(2, 0, SC)
+        quantise_windows(0, half, widths[0])
+        multiply(0, 0, 0, half)
+        multiply(0, 0, half, widths[0])
+        group_window_words(0, 1, SC)
+        group_window_words(1, 1, VE)
+        group_grad_words(1)
+        group_grad_words(2)
+        quantise_grad(1)
+        quantise_grad(2)
+        multiply(0, 1)
+        multiply(0, 2)
+        group_window_words(2, 1, SC)
+        quantise_windows(1)
+        copy_out(0, 0, SC)
+        store(0, 0, 0)
+        copy_out(0, 1, SC)
+        store(0, 0, 1)
+        group_window_words(1, 2, VE)
+        group_window_words(0, 2, VE)
+        group_window_words(2, 2, VE)
+        quantise_windows(2)
+        copy_out(0, 2, SC)
+        store(0, 0, 2)
         for ot in range(O_TILES):
-            multiply_and_store(0, ot)
-        for ot in range(O_TILES):
-            for grp in range(1, len(groups)):
-                multiply_and_store(grp, ot)
+            multiply(1, ot)
+            multiply(2, ot)
+            copy_out(1, ot, ot % 2 == 1)
+            copy_out(2, ot, ot % 2 == 0)
+            store(1, 2, ot)

@@ -235,16 +235,16 @@ def tile_model_pa_s_kernel(tc, x, grad_output, out):
         quantise_grad(2)
         multiply(0, 1)
         multiply(0, 2)
+        group_window_words(1, 2, VE)
+        group_window_words(0, 2, VE)
         group_window_words(2, 1, SC)
+        group_window_words(2, 2, VE)
         quantise_windows(1)
+        quantise_windows(2)
         copy_out(0, 0, SC)
         store(0, 0, 0)
         copy_out(0, 1, SC)
         store(0, 0, 1)
-        group_window_words(1, 2, VE)
-        group_window_words(0, 2, VE)
-        group_window_words(2, 2, VE)
-        quantise_windows(2)
         copy_out(0, 2, SC)
         store(0, 0, 2)
         for ot in range(O_TILES):

@@ -21,7 +21,6 @@ CH_PER_BANK = BANK // TAPS
 PASS_WIDTHS = (128, 256, 512)
 PSUM_BANKS = 8
 IDLE_MATMULS_HEAD = 4
-IDLE_MATMULS_MID = 2
 
 FLOPS = 2 * C_OUT * C_IN * TAPS * N_IMG * HO * WO
 
@@ -219,7 +218,6 @@ def tile_model_pa_s_kernel(tc, x, grad_output, out):
         group_window_words(1, 0, VE)
         split_grad_rows(2)
         transpose_grad_rows(2)
-        multiply_zeros(IDLE_MATMULS_MID)
         group_grad_words(0)
         quantise_grad(0)
         quantise_windows(0, 0, half)

@@ -17,9 +17,15 @@ ROW_PAIRS = HO // 2
 ROW_SETS = KH + 1
 O_TILES = C_OUT // P
 BANK = 512
-CH_PER_BANK = BANK // TAPS
-PASS_WIDTHS = (128, 256, 512)
 PSUM_BANKS = 8
+C_A = BANK // TAPS
+A_COLS = 512
+C_B = C_IN - C_A
+B_BANKS = 2
+C_B_BANK = C_B // B_BANKS
+B_SLICE = 128
+B_KW_COLS = B_BANKS * B_SLICE
+B_KW_ORDER = (0, 2, 1)
 IDLE_MATMULS_HEAD = 4
 
 FLOPS = 2 * C_OUT * C_IN * TAPS * N_IMG * HO * WO
@@ -27,9 +33,6 @@ FLOPS = 2 * C_OUT * C_IN * TAPS * N_IMG * HO * WO
 
 def tile_model_pa_s_kernel(tc, x, grad_output, out):
     nc = tc.nc
-
-    groups = [(c0, min(CH_PER_BANK, C_IN - c0)) for c0 in range(0, C_IN, CH_PER_BANK)]
-    widths = [min(n for n in PASS_WIDTHS if n >= TAPS * cg) for (c0, cg) in groups]
 
     with tc.tile_pool(name="keep", bufs=1) as keep, tc.tile_pool(
         name="results", bufs=2 * O_TILES
@@ -67,13 +70,14 @@ def tile_model_pa_s_kernel(tc, x, grad_output, out):
         ident = keep.tile([P, P], F32)
         make_identity(nc, ident[:])
 
-        x_grouped, x_codes, x_scales = [], [], []
-        for grp, (c0, cg) in enumerate(groups):
-            grouped = keep.tile([P, 4 * widths[grp]], BF16, align_bytes=64, name="x_grouped%d" % grp)
-            nc.vector.memset(grouped[:, 4 * TAPS * cg :], 0.0)
-            x_grouped.append(grouped)
-            x_codes.append(keep.tile([P, widths[grp]], U32, align_bytes=64, name="x_codes%d" % grp))
-            x_scales.append(keep.tile([P, widths[grp]], U8, align_bytes=64, name="x_scales%d" % grp))
+        a_grouped = keep.tile([P, 4 * A_COLS], BF16, align_bytes=64)
+        a_codes = keep.tile([P, A_COLS], U32, align_bytes=64)
+        a_scales = keep.tile([P, A_COLS], U8, align_bytes=64)
+        nc.vector.memset(a_grouped[:, 4 * TAPS * C_A :], 0.0)
+        b_grouped = keep.tile([P, KW, B_BANKS, 4 * B_SLICE], BF16, align_bytes=64)
+        b_codes = keep.tile([P, KW * B_KW_COLS], U32, align_bytes=64)
+        b_scales = keep.tile([P, KW * B_KW_COLS], U8, align_bytes=64)
+        nc.vector.memset(b_grouped[:, :, :, 4 * KH * C_B_BANK :], 0.0)
         g_grouped = [
             keep.tile([P, 4 * P], BF16, align_bytes=64, name="g_grouped%d" % ot) for ot in range(O_TILES)
         ]
@@ -111,36 +115,51 @@ def tile_model_pa_s_kernel(tc, x, grad_output, out):
                     out=x_t[kw][:, r, :], in_=row_set.rearrange("c m n w -> c (m n w)"), identity=ident[:]
                 )
 
-        def group_window_words(kw, grp, on_scalar):
-            c0, cg = groups[grp]
-            grouped_words = x_grouped[grp][:].bitcast(F32)[:, 0 : 2 * TAPS * cg].rearrange(
+        def group_a_words(kw, on_scalar):
+            words = a_grouped[:].bitcast(F32)[:, 0 : 2 * TAPS * C_A].rearrange(
                 "p (kw kh c u) -> p kw kh c u", kh=KH, kw=KW, u=2
             )
             copy(
                 on_scalar,
-                grouped_words[:, kw, 0:KH:2, :, :],
-                x_t[kw][:, :, c0 : c0 + cg].rearrange("p (a u) c -> p a c u", u=2),
+                words[:, kw, 0:KH:2, :, :],
+                x_t[kw][:, :, 0:C_A].rearrange("p (a u) c -> p a c u", u=2),
+            )
+            copy(on_scalar, words[:, kw, 1, :, :], x_t[kw][:, 1:3, 0:C_A].rearrange("p u c -> p c u"))
+
+        def group_b_words(kw, on_scalar):
+            words = b_grouped[:, kw, :, :].bitcast(F32)[:, :, 0 : 2 * KH * C_B_BANK].rearrange(
+                "p s (kh c u) -> p s kh c u", kh=KH, u=2
             )
             copy(
                 on_scalar,
-                grouped_words[:, kw, 1, :, :],
-                x_t[kw][:, 1:3, c0 : c0 + cg].rearrange("p u c -> p c u"),
+                words[:, :, 0:KH:2, :, :],
+                x_t[kw][:, :, C_A:].rearrange("p (a u) (s c) -> p s a c u", u=2, s=B_BANKS),
+            )
+            copy(
+                on_scalar,
+                words[:, :, 1, :, :],
+                x_t[kw][:, 1:3, C_A:].rearrange("p u (s c) -> p s c u", s=B_BANKS),
             )
 
-        def quantise_windows(grp, lo=0, hi=None):
-            hi = widths[grp] if hi is None else hi
+        def quantise_a(lo, hi):
             nc.vector.quantize_mx(
-                out=x_codes[grp][:, lo:hi].bitcast(FP8X4),
-                scales=x_scales[grp][:, lo:hi],
-                in_=x_grouped[grp][:, 4 * lo : 4 * hi],
+                out=a_codes[:, lo:hi].bitcast(FP8X4), scales=a_scales[:, lo:hi], in_=a_grouped[:, 4 * lo : 4 * hi]
+            )
+
+        def quantise_b(kw):
+            cols = slice(kw * B_KW_COLS, (kw + 1) * B_KW_COLS)
+            nc.vector.quantize_mx(
+                out=b_codes[:, cols].bitcast(FP8X4),
+                scales=b_scales[:, cols],
+                in_=b_grouped[:, kw, :, :].rearrange("p s k -> p (s k)"),
             )
 
         g_row_sets = [keep.tile([P, 2, P], F32, name="g_row_sets%d" % ot) for ot in range(O_TILES)]
         g_t = {}
 
-        def split_grad_rows(ot):
+        def split_grad_rows(ot, on_scalar):
             copy(
-                ot == 0,
+                on_scalar,
                 g_row_sets[ot][:].rearrange("o u (m n w) -> o u m n w", n=N_IMG, w=WO_WORDS),
                 g_in[ot][:].bitcast(F32).rearrange("o (n m u w) -> o u m n w", n=N_IMG, u=2, w=WO_WORDS),
             )
@@ -150,10 +169,11 @@ def tile_model_pa_s_kernel(tc, x, grad_output, out):
             for u in range(2):
                 nc.tensor.transpose(out=g_t[ot][:, u, :], in_=g_row_sets[ot][:, u, :], identity=ident[:])
 
-        def group_grad_words(ot):
-            nc.scalar.copy(
-                out=g_grouped[ot][:].bitcast(F32).rearrange("p (o u) -> p o u", u=2),
-                in_=g_t[ot][:].rearrange("p u o -> p o u"),
+        def group_grad_words(ot, on_scalar):
+            copy(
+                on_scalar,
+                g_grouped[ot][:].bitcast(F32).rearrange("p (o u) -> p o u", u=2),
+                g_t[ot][:].rearrange("p u o -> p o u"),
             )
 
         def quantise_grad(ot):
@@ -162,92 +182,106 @@ def tile_model_pa_s_kernel(tc, x, grad_output, out):
                 out=g_codes[:, o_cols].bitcast(FP8X4), scales=g_scales[:, o_cols], in_=g_grouped[ot][:]
             )
 
-        accs = {}
-        res_tiles = {}
-
-        def multiply(grp, ot, lo=0, hi=None):
-            hi = widths[grp] if hi is None else hi
+        def one_pass(ot, acc, codes, scales):
             o_cols = slice(ot * P, (ot + 1) * P)
-            if lo == 0:
-                accs[(grp, ot)] = psum.tile([P, BANK], F32, tag="bank", name="acc")
             nc.tensor.matmul_mx(
-                out=accs[(grp, ot)][:, lo:hi],
+                out=acc,
                 lhsT=g_codes[:, o_cols].bitcast(FP8X4),
                 lhsT_scale=g_scales[:, o_cols],
-                rhs=x_codes[grp][:, lo:hi].bitcast(FP8X4),
-                rhs_scale=x_scales[grp][:, lo:hi],
+                rhs=codes.bitcast(FP8X4),
+                rhs_scale=scales,
                 start=True,
                 stop=True,
             )
 
-        def copy_out(grp, ot, on_scalar):
-            c0, cg = groups[grp]
-            first_c = groups[min(grp, 1)][0]
-            if grp <= 1:
-                res_tiles[ot] = results.tile([P, TAPS * (C_IN - CH_PER_BANK)], F32, name="res")
+        accs = {}
+
+        def multiply_a(ot, lo, hi):
+            if lo == 0:
+                accs[("a", ot)] = psum.tile([P, BANK], F32, tag="bank", name="acc_a")
+            one_pass(ot, accs[("a", ot)][:, lo:hi], a_codes[:, lo:hi], a_scales[:, lo:hi])
+
+        def multiply_b(ot):
+            for s in range(B_BANKS):
+                accs[("b", ot, s)] = psum.tile([P, KW, B_SLICE], F32, tag="bank", name="acc_b")
+            for kw in B_KW_ORDER:
+                for s in range(B_BANKS):
+                    lo = kw * B_KW_COLS + s * B_SLICE
+                    one_pass(
+                        ot,
+                        accs[("b", ot, s)][:, kw, :],
+                        b_codes[:, lo : lo + B_SLICE],
+                        b_scales[:, lo : lo + B_SLICE],
+                    )
+
+        def store(ot, first_c, end_c, res):
+            nc.sync.dma_start(
+                out=out[ot * P : (ot + 1) * P, first_c:end_c].rearrange("o c kh kw -> o (c kh kw)"), in_=res
+            )
+
+        def finish_a(ot, on_scalar):
+            res = results.tile([P, TAPS * C_B], F32, name="res")
             copy(
                 on_scalar,
-                res_tiles[ot][:, TAPS * (c0 - first_c) : TAPS * (c0 + cg - first_c)].rearrange(
-                    "o (c kh kw) -> o c kh kw", kh=KH, kw=KW
-                ),
-                accs[(grp, ot)][:, 0 : TAPS * cg].rearrange("o (kw kh c) -> o c kh kw", kh=KH, kw=KW),
+                res[:, 0 : TAPS * C_A].rearrange("o (c kh kw) -> o c kh kw", kh=KH, kw=KW),
+                accs[("a", ot)][:, 0 : TAPS * C_A].rearrange("o (kw kh c) -> o c kh kw", kh=KH, kw=KW),
             )
+            store(ot, 0, C_A, res[:, 0 : TAPS * C_A])
 
-        def store(first_grp, last_grp, ot):
-            first_c = groups[first_grp][0]
-            end_c = groups[last_grp][0] + groups[last_grp][1]
-            nc.sync.dma_start(
-                out=out[ot * P : (ot + 1) * P, first_c:end_c].rearrange("o c kh kw -> o (c kh kw)"),
-                in_=res_tiles[ot][:, 0 : TAPS * (end_c - first_c)],
-            )
+        def finish_b(ot, on_scalar):
+            res = results.tile([P, TAPS * C_B], F32, name="res")
+            for s in range(B_BANKS):
+                copy(
+                    on_scalar[s],
+                    res[:, TAPS * C_B_BANK * s : TAPS * C_B_BANK * (s + 1)].rearrange(
+                        "o (c kh kw) -> o c kh kw", kh=KH, kw=KW
+                    ),
+                    accs[("b", ot, s)][:, :, 0 : KH * C_B_BANK].rearrange("o kw (kh c) -> o c kh kw", kh=KH),
+                )
+            store(ot, C_A, C_IN, res[:])
 
         SC, VE = True, False
-        half = widths[0] // 2
+        half = A_COLS // 2
         multiply_zeros(IDLE_MATMULS_HEAD)
         gather_window_rows(0)
         gather_window_rows(1)
         transpose_window_rows(0)
+        split_grad_rows(0, VE)
+        transpose_grad_rows(0)
         gather_window_rows(2)
         transpose_window_rows(1)
-        split_grad_rows(0)
-        transpose_grad_rows(0)
         transpose_window_rows(2)
-        split_grad_rows(1)
+        split_grad_rows(1, VE)
+        split_grad_rows(2, SC)
         transpose_grad_rows(1)
-        group_window_words(0, 0, SC)
-        group_window_words(1, 0, VE)
-        split_grad_rows(2)
         transpose_grad_rows(2)
-        group_grad_words(0)
+        group_a_words(0, SC)
+        group_grad_words(0, VE)
+        group_b_words(0, SC)
+        group_a_words(1, VE)
+        group_a_words(2, SC)
         quantise_grad(0)
-        quantise_windows(0, 0, half)
-        group_window_words(2, 0, SC)
-        quantise_windows(0, half, widths[0])
-        multiply(0, 0, 0, half)
-        multiply(0, 0, half, widths[0])
-        group_window_words(0, 1, SC)
-        group_window_words(1, 1, VE)
-        group_grad_words(1)
-        group_grad_words(2)
+        quantise_a(0, half)
+        quantise_a(half, A_COLS)
+        multiply_a(0, 0, half)
+        multiply_a(0, half, A_COLS)
+        group_grad_words(1, SC)
         quantise_grad(1)
+        multiply_a(1, 0, A_COLS)
+        group_b_words(2, SC)
+        group_b_words(1, SC)
+        quantise_b(0)
+        quantise_b(2)
+        quantise_b(1)
+        group_grad_words(2, VE)
+        finish_a(0, SC)
+        finish_a(1, SC)
         quantise_grad(2)
-        multiply(0, 1)
-        multiply(0, 2)
-        group_window_words(1, 2, VE)
-        group_window_words(0, 2, VE)
-        group_window_words(2, 1, SC)
-        group_window_words(2, 2, VE)
-        quantise_windows(1)
-        quantise_windows(2)
-        copy_out(0, 0, SC)
-        store(0, 0, 0)
-        copy_out(0, 1, SC)
-        store(0, 0, 1)
-        copy_out(0, 2, SC)
-        store(0, 0, 2)
-        for ot in range(O_TILES):
-            multiply(1, ot)
-            multiply(2, ot)
-            copy_out(1, ot, ot % 2 == 1)
-            copy_out(2, ot, ot % 2 == 0)
-            store(1, 2, ot)
+        multiply_b(0)
+        finish_b(0, (SC, VE))
+        multiply_b(1)
+        finish_b(1, (SC, VE))
+        multiply_a(2, 0, A_COLS)
+        finish_a(2, SC)
+        multiply_b(2)
+        finish_b(2, (VE, VE))

@@ -18,14 +18,13 @@ ROW_SETS = KH + 1
 O_TILES = C_OUT // P
 BANK = 512
 PSUM_BANKS = 8
-C_A = BANK // TAPS
-A_COLS = 512
-C_B = C_IN - C_A
-B_BANKS = 2
-C_B_BANK = C_B // B_BANKS
-B_SLICE = 128
-B_KW_COLS = B_BANKS * B_SLICE
-B_KW_ORDER = (0, 2, 1)
+C_S = 40
+S_GROUPS = (0, C_S)
+SLICE = 128
+C_L = C_IN - 2 * C_S
+L_FIRST = 2 * C_S
+L_COLS = 512
+KW_ORDER = (0, 2, 1)
 IDLE_MATMULS_HEAD = 4
 
 FLOPS = 2 * C_OUT * C_IN * TAPS * N_IMG * HO * WO
@@ -70,14 +69,17 @@ def tile_model_pa_s_kernel(tc, x, grad_output, out):
         ident = keep.tile([P, P], F32)
         make_identity(nc, ident[:])
 
-        a_grouped = keep.tile([P, 4 * A_COLS], BF16, align_bytes=64)
-        a_codes = keep.tile([P, A_COLS], U32, align_bytes=64)
-        a_scales = keep.tile([P, A_COLS], U8, align_bytes=64)
-        nc.vector.memset(a_grouped[:, 4 * TAPS * C_A :], 0.0)
-        b_grouped = keep.tile([P, KW, B_BANKS, 4 * B_SLICE], BF16, align_bytes=64)
-        b_codes = keep.tile([P, KW * B_KW_COLS], U32, align_bytes=64)
-        b_scales = keep.tile([P, KW * B_KW_COLS], U8, align_bytes=64)
-        nc.vector.memset(b_grouped[:, :, :, 4 * KH * C_B_BANK :], 0.0)
+        s_grouped, s_codes, s_scales = [], [], []
+        for grp in range(len(S_GROUPS)):
+            grouped = keep.tile([P, KW, 4 * SLICE], BF16, align_bytes=64, name="s_grouped%d" % grp)
+            nc.vector.memset(grouped[:, :, 4 * KH * C_S :], 0.0)
+            s_grouped.append(grouped)
+            s_codes.append(keep.tile([P, KW * SLICE], U32, align_bytes=64, name="s_codes%d" % grp))
+            s_scales.append(keep.tile([P, KW * SLICE], U8, align_bytes=64, name="s_scales%d" % grp))
+        l_grouped = keep.tile([P, 4 * L_COLS], BF16, align_bytes=64)
+        l_codes = keep.tile([P, L_COLS], U32, align_bytes=64)
+        l_scales = keep.tile([P, L_COLS], U8, align_bytes=64)
+        nc.vector.memset(l_grouped[:, 4 * TAPS * C_L :], 0.0)
         g_grouped = [
             keep.tile([P, 4 * P], BF16, align_bytes=64, name="g_grouped%d" % ot) for ot in range(O_TILES)
         ]
@@ -115,43 +117,30 @@ def tile_model_pa_s_kernel(tc, x, grad_output, out):
                     out=x_t[kw][:, r, :], in_=row_set.rearrange("c m n w -> c (m n w)"), identity=ident[:]
                 )
 
-        def group_a_words(kw, on_scalar):
-            words = a_grouped[:].bitcast(F32)[:, 0 : 2 * TAPS * C_A].rearrange(
-                "p (kw kh c u) -> p kw kh c u", kh=KH, kw=KW, u=2
-            )
-            copy(
-                on_scalar,
-                words[:, kw, 0:KH:2, :, :],
-                x_t[kw][:, :, 0:C_A].rearrange("p (a u) c -> p a c u", u=2),
-            )
-            copy(on_scalar, words[:, kw, 1, :, :], x_t[kw][:, 1:3, 0:C_A].rearrange("p u c -> p c u"))
+        def group_words(dst, kw, first_c, channels, on_scalar):
+            words = dst.bitcast(F32)[:, 0 : 2 * KH * channels].rearrange("p (kh c u) -> p kh c u", kh=KH, u=2)
+            rows = x_t[kw][:, :, first_c : first_c + channels]
+            copy(on_scalar, words[:, 0:KH:2, :, :], rows.rearrange("p (a u) c -> p a c u", u=2))
+            copy(on_scalar, words[:, 1, :, :], rows[:, 1:3, :].rearrange("p u c -> p c u"))
 
-        def group_b_words(kw, on_scalar):
-            words = b_grouped[:, kw, :, :].bitcast(F32)[:, :, 0 : 2 * KH * C_B_BANK].rearrange(
-                "p s (kh c u) -> p s kh c u", kh=KH, u=2
-            )
-            copy(
-                on_scalar,
-                words[:, :, 0:KH:2, :, :],
-                x_t[kw][:, :, C_A:].rearrange("p (a u) (s c) -> p s a c u", u=2, s=B_BANKS),
-            )
-            copy(
-                on_scalar,
-                words[:, :, 1, :, :],
-                x_t[kw][:, 1:3, C_A:].rearrange("p u (s c) -> p s c u", s=B_BANKS),
-            )
+        def group_small(grp, kw, on_scalar):
+            group_words(s_grouped[grp][:, kw, :], kw, S_GROUPS[grp], C_S, on_scalar)
 
-        def quantise_a(lo, hi):
+        def group_large(kw, on_scalar):
+            width = 4 * KH * C_L
+            group_words(l_grouped[:, kw * width : (kw + 1) * width], kw, L_FIRST, C_L, on_scalar)
+
+        def quantise_small(grp, kw):
+            cols = slice(kw * SLICE, (kw + 1) * SLICE)
             nc.vector.quantize_mx(
-                out=a_codes[:, lo:hi].bitcast(FP8X4), scales=a_scales[:, lo:hi], in_=a_grouped[:, 4 * lo : 4 * hi]
+                out=s_codes[grp][:, cols].bitcast(FP8X4),
+                scales=s_scales[grp][:, cols],
+                in_=s_grouped[grp][:, kw, :],
             )
 
-        def quantise_b(kw):
-            cols = slice(kw * B_KW_COLS, (kw + 1) * B_KW_COLS)
+        def quantise_large(lo, hi):
             nc.vector.quantize_mx(
-                out=b_codes[:, cols].bitcast(FP8X4),
-                scales=b_scales[:, cols],
-                in_=b_grouped[:, kw, :, :].rearrange("p s k -> p (s k)"),
+                out=l_codes[:, lo:hi].bitcast(FP8X4), scales=l_scales[:, lo:hi], in_=l_grouped[:, 4 * lo : 4 * hi]
             )
 
         g_row_sets = [keep.tile([P, 2, P], F32, name="g_row_sets%d" % ot) for ot in range(O_TILES)]
@@ -196,92 +185,99 @@ def tile_model_pa_s_kernel(tc, x, grad_output, out):
 
         accs = {}
 
-        def multiply_a(ot, lo, hi):
-            if lo == 0:
-                accs[("a", ot)] = psum.tile([P, BANK], F32, tag="bank", name="acc_a")
-            one_pass(ot, accs[("a", ot)][:, lo:hi], a_codes[:, lo:hi], a_scales[:, lo:hi])
+        def multiply_small(grp, ot):
+            accs[(grp, ot)] = psum.tile([P, KW, SLICE], F32, tag="bank", name="acc_small")
+            for kw in KW_ORDER:
+                cols = slice(kw * SLICE, (kw + 1) * SLICE)
+                one_pass(ot, accs[(grp, ot)][:, kw, :], s_codes[grp][:, cols], s_scales[grp][:, cols])
 
-        def multiply_b(ot):
-            for s in range(B_BANKS):
-                accs[("b", ot, s)] = psum.tile([P, KW, B_SLICE], F32, tag="bank", name="acc_b")
-            for kw in B_KW_ORDER:
-                for s in range(B_BANKS):
-                    lo = kw * B_KW_COLS + s * B_SLICE
-                    one_pass(
-                        ot,
-                        accs[("b", ot, s)][:, kw, :],
-                        b_codes[:, lo : lo + B_SLICE],
-                        b_scales[:, lo : lo + B_SLICE],
-                    )
+        def multiply_large(ot):
+            accs[("large", ot)] = psum.tile([P, L_COLS], F32, tag="bank", name="acc_large")
+            one_pass(ot, accs[("large", ot)][:], l_codes[:], l_scales[:])
 
         def store(ot, first_c, end_c, res):
             nc.sync.dma_start(
                 out=out[ot * P : (ot + 1) * P, first_c:end_c].rearrange("o c kh kw -> o (c kh kw)"), in_=res
             )
 
-        def finish_a(ot, on_scalar):
-            res = results.tile([P, TAPS * C_B], F32, name="res")
+        small_res = {}
+
+        def copy_out_small(grp, ot, on_scalar):
+            if grp == 0:
+                small_res[ot] = results.tile([P, TAPS * L_FIRST], F32, name="small_res")
+            first = TAPS * S_GROUPS[grp]
             copy(
                 on_scalar,
-                res[:, 0 : TAPS * C_A].rearrange("o (c kh kw) -> o c kh kw", kh=KH, kw=KW),
-                accs[("a", ot)][:, 0 : TAPS * C_A].rearrange("o (kw kh c) -> o c kh kw", kh=KH, kw=KW),
+                small_res[ot][:, first : first + TAPS * C_S].rearrange("o (c kh kw) -> o c kh kw", kh=KH, kw=KW),
+                accs[(grp, ot)][:, :, 0 : KH * C_S].rearrange("o kw (kh c) -> o c kh kw", kh=KH),
             )
-            store(ot, 0, C_A, res[:, 0 : TAPS * C_A])
 
-        def finish_b(ot, on_scalar):
-            res = results.tile([P, TAPS * C_B], F32, name="res")
-            for s in range(B_BANKS):
-                copy(
-                    on_scalar[s],
-                    res[:, TAPS * C_B_BANK * s : TAPS * C_B_BANK * (s + 1)].rearrange(
-                        "o (c kh kw) -> o c kh kw", kh=KH, kw=KW
-                    ),
-                    accs[("b", ot, s)][:, :, 0 : KH * C_B_BANK].rearrange("o kw (kh c) -> o c kh kw", kh=KH),
-                )
-            store(ot, C_A, C_IN, res[:])
+        def store_small(first_grp, last_grp, ot):
+            first_c, end_c = S_GROUPS[first_grp], S_GROUPS[last_grp] + C_S
+            store(ot, first_c, end_c, small_res[ot][:, TAPS * first_c : TAPS * end_c])
+
+        def finish_large(ot, on_scalar):
+            res = results.tile([P, TAPS * C_L], F32, name="large_res")
+            copy(
+                on_scalar,
+                res[:].rearrange("o (c kh kw) -> o c kh kw", kh=KH, kw=KW),
+                accs[("large", ot)][:, 0 : TAPS * C_L].rearrange("o (kw kh c) -> o c kh kw", kh=KH, kw=KW),
+            )
+            store(ot, L_FIRST, C_IN, res[:])
 
         SC, VE = True, False
-        half = A_COLS // 2
+        half = L_COLS // 2
         multiply_zeros(IDLE_MATMULS_HEAD)
         gather_window_rows(0)
         gather_window_rows(1)
         transpose_window_rows(0)
         split_grad_rows(0, VE)
-        transpose_grad_rows(0)
         gather_window_rows(2)
-        transpose_window_rows(1)
         transpose_window_rows(2)
+        transpose_grad_rows(0)
         split_grad_rows(1, VE)
-        split_grad_rows(2, SC)
+        split_grad_rows(2, VE)
+        transpose_window_rows(1)
         transpose_grad_rows(1)
         transpose_grad_rows(2)
-        group_a_words(0, SC)
-        group_grad_words(0, VE)
-        group_b_words(0, SC)
-        group_a_words(1, VE)
-        group_a_words(2, SC)
-        quantise_grad(0)
-        quantise_a(0, half)
-        quantise_a(half, A_COLS)
-        multiply_a(0, 0, half)
-        multiply_a(0, half, A_COLS)
+        group_small(0, 0, SC)
+        group_small(1, 0, SC)
+        group_small(0, 2, VE)
+        group_small(1, 2, VE)
+        group_grad_words(0, SC)
+        group_small(0, 1, SC)
         group_grad_words(1, SC)
+        group_small(1, 1, SC)
+        quantise_small(0, 0)
+        quantise_small(0, 2)
+        quantise_grad(0)
+        quantise_small(0, 1)
         quantise_grad(1)
-        multiply_a(1, 0, A_COLS)
-        group_b_words(2, SC)
-        group_b_words(1, SC)
-        quantise_b(0)
-        quantise_b(2)
-        quantise_b(1)
-        group_grad_words(2, VE)
-        finish_a(0, SC)
-        finish_a(1, SC)
+        multiply_small(0, 0)
+        multiply_small(0, 1)
+        group_grad_words(2, SC)
+        for kw in range(KW):
+            group_large(kw, SC)
+        for kw in KW_ORDER:
+            quantise_small(1, kw)
+        multiply_small(1, 0)
+        multiply_small(1, 1)
+        copy_out_small(0, 0, VE)
+        store_small(0, 0, 0)
         quantise_grad(2)
-        multiply_b(0)
-        finish_b(0, (SC, VE))
-        multiply_b(1)
-        finish_b(1, (SC, VE))
-        multiply_a(2, 0, A_COLS)
-        finish_a(2, SC)
-        multiply_b(2)
-        finish_b(2, (VE, VE))
+        quantise_large(0, half)
+        quantise_large(half, L_COLS)
+        copy_out_small(0, 1, SC)
+        store_small(0, 0, 1)
+        copy_out_small(1, 0, SC)
+        store_small(1, 1, 0)
+        copy_out_small(1, 1, VE)
+        store_small(1, 1, 1)
+        multiply_small(0, 2)
+        copy_out_small(0, 2, SC)
+        multiply_small(1, 2)
+        copy_out_small(1, 2, VE)
+        store_small(0, 1, 2)
+        for ot in range(O_TILES):
+            multiply_large(ot)
+            finish_large(ot, ot % 2 == 0)

@@ -231,8 +231,8 @@ def tile_model_pa_s_kernel(tc, x, grad_output, out):
         gather_window_rows(0)
         gather_window_rows(1)
         transpose_window_rows(0)
-        split_grad_rows(0, VE)
         gather_window_rows(2)
+        split_grad_rows(0, VE)
         transpose_window_rows(2)
         transpose_grad_rows(0)
         split_grad_rows(1, VE)

@@ -233,51 +233,51 @@ def tile_model_pa_s_kernel(tc, x, grad_output, out):
         transpose_window_rows(0)
         gather_window_rows(2)
         split_grad_rows(0, VE)
-        transpose_window_rows(2)
         transpose_grad_rows(0)
+        transpose_window_rows(2)
+        transpose_window_rows(1)
         split_grad_rows(1, VE)
         split_grad_rows(2, VE)
-        transpose_window_rows(1)
         transpose_grad_rows(1)
         transpose_grad_rows(2)
         group_small(0, 0, SC)
+        group_grad_words(0, VE)
         group_small(1, 0, SC)
-        group_small(0, 2, VE)
-        group_small(1, 2, VE)
-        group_grad_words(0, SC)
-        group_small(0, 1, SC)
-        group_grad_words(1, SC)
-        group_small(1, 1, SC)
+        group_small(0, 2, SC)
+        group_small(1, 2, SC)
         quantise_small(0, 0)
-        quantise_small(0, 2)
         quantise_grad(0)
+        group_small(0, 1, VE)
+        quantise_small(0, 2)
         quantise_small(0, 1)
-        quantise_grad(1)
         multiply_small(0, 0)
-        multiply_small(0, 1)
+        group_grad_words(1, SC)
         group_grad_words(2, SC)
-        for kw in range(KW):
-            group_large(kw, SC)
-        for kw in KW_ORDER:
-            quantise_small(1, kw)
-        multiply_small(1, 0)
-        multiply_small(1, 1)
-        copy_out_small(0, 0, VE)
-        store_small(0, 0, 0)
+        quantise_grad(1)
+        multiply_small(0, 1)
+        group_small(1, 1, SC)
+        group_large(1, SC)
+        quantise_small(1, 0)
         quantise_grad(2)
-        quantise_large(0, half)
+        multiply_small(0, 2)
+        quantise_small(1, 2)
+        quantise_small(1, 1)
+        for ot in range(O_TILES):
+            copy_out_small(0, ot, SC)
+            store_small(0, 0, ot)
+        multiply_small(1, 0)
+        group_large(2, VE)
+        group_large(0, VE)
         quantise_large(half, L_COLS)
-        copy_out_small(0, 1, SC)
-        store_small(0, 0, 1)
+        quantise_large(0, half)
         copy_out_small(1, 0, SC)
         store_small(1, 1, 0)
-        copy_out_small(1, 1, VE)
+        multiply_small(1, 1)
+        copy_out_small(1, 1, SC)
         store_small(1, 1, 1)
-        multiply_small(0, 2)
-        copy_out_small(0, 2, SC)
         multiply_small(1, 2)
         copy_out_small(1, 2, VE)
-        store_small(0, 1, 2)
+        store_small(1, 1, 2)
         for ot in range(O_TILES):
             multiply_large(ot)
             finish_large(ot, ot % 2 == 0)

@@ -33,9 +33,7 @@ FLOPS = 2 * C_OUT * C_IN * TAPS * N_IMG * HO * WO
 def tile_model_pa_s_kernel(tc, x, grad_output, out):
     nc = tc.nc
 
-    with tc.tile_pool(name="keep", bufs=1) as keep, tc.tile_pool(
-        name="results", bufs=2 * O_TILES
-    ) as results, tc.psum_pool(name="psum", bufs=PSUM_BANKS - KW) as psum, tc.manual_schedule():
+    with tc.tile_pool(name="keep", bufs=1) as keep, tc.psum_pool(name="psum", bufs=PSUM_BANKS - KW) as psum, tc.manual_schedule():
 
         def copy(on_scalar, dst, src):
             if on_scalar:
@@ -195,35 +193,38 @@ def tile_model_pa_s_kernel(tc, x, grad_output, out):
             accs[("large", ot)] = psum.tile([P, L_COLS], F32, tag="bank", name="acc_large")
             one_pass(ot, accs[("large", ot)][:], l_codes[:], l_scales[:])
 
-        def store(ot, first_c, end_c, res):
+        res_small = [keep.tile([P, n, TAPS * L_FIRST], F32, name="res_small%d" % n) for n in (1, O_TILES - 1)]
+        res_large = [keep.tile([P, n, TAPS * C_L], F32, name="res_large%d" % n) for n in (1, O_TILES - 1)]
+
+        def store(first_ot, last_ot, first_c, end_c, res):
             nc.sync.dma_start(
-                out=out[ot * P : (ot + 1) * P, first_c:end_c].rearrange("o c kh kw -> o (c kh kw)"), in_=res
+                out=out[first_ot * P : (last_ot + 1) * P, first_c:end_c].rearrange(
+                    "(s o) c kh kw -> o s (c kh kw)", o=P
+                ),
+                in_=res,
             )
 
-        small_res = {}
-
         def copy_out_small(grp, ot, on_scalar):
-            if grp == 0:
-                small_res[ot] = results.tile([P, TAPS * L_FIRST], F32, name="small_res")
             first = TAPS * S_GROUPS[grp]
             copy(
                 on_scalar,
-                small_res[ot][:, first : first + TAPS * C_S].rearrange("o (c kh kw) -> o c kh kw", kh=KH, kw=KW),
+                res_small[min(ot, 1)][:, max(ot - 1, 0), first : first + TAPS * C_S].rearrange(
+                    "o (c kh kw) -> o c kh kw", kh=KH, kw=KW
+                ),
                 accs[(grp, ot)][:, :, 0 : KH * C_S].rearrange("o kw (kh c) -> o c kh kw", kh=KH),
             )
 
-        def store_small(first_grp, last_grp, ot):
-            first_c, end_c = S_GROUPS[first_grp], S_GROUPS[last_grp] + C_S
-            store(ot, first_c, end_c, small_res[ot][:, TAPS * first_c : TAPS * end_c])
+        def store_small(grp, first_ot, last_ot):
+            first_c, end_c = S_GROUPS[grp], S_GROUPS[grp] + C_S
+            s = slice(max(first_ot - 1, 0), max(last_ot - 1, 0) + 1)
+            store(first_ot, last_ot, first_c, end_c, res_small[min(first_ot, 1)][:, s, TAPS * first_c : TAPS * end_c])
 
-        def finish_large(ot, on_scalar):
-            res = results.tile([P, TAPS * C_L], F32, name="large_res")
+        def copy_out_large(ot, on_scalar):
             copy(
                 on_scalar,
-                res[:].rearrange("o (c kh kw) -> o c kh kw", kh=KH, kw=KW),
+                res_large[min(ot, 1)][:, max(ot - 1, 0), :].rearrange("o (c kh kw) -> o c kh kw", kh=KH, kw=KW),
                 accs[("large", ot)][:, 0 : TAPS * C_L].rearrange("o (kw kh c) -> o c kh kw", kh=KH, kw=KW),
             )
-            store(ot, L_FIRST, C_IN, res[:])
 
         SC, VE = True, False
         half = L_COLS // 2
@@ -264,20 +265,21 @@ def tile_model_pa_s_kernel(tc, x, grad_output, out):
         quantise_small(1, 1)
         for ot in range(O_TILES):
             copy_out_small(0, ot, SC)
-            store_small(0, 0, ot)
+            store_small(0, ot, ot)
         multiply_small(1, 0)
         group_large(2, VE)
         group_large(0, VE)
         quantise_large(half, L_COLS)
         quantise_large(0, half)
         copy_out_small(1, 0, SC)
-        store_small(1, 1, 0)
+        store_small(1, 0, 0)
         multiply_small(1, 1)
         copy_out_small(1, 1, SC)
-        store_small(1, 1, 1)
         multiply_small(1, 2)
         copy_out_small(1, 2, VE)
         store_small(1, 1, 2)
         for ot in range(O_TILES):
             multiply_large(ot)
-            finish_large(ot, ot % 2 == 0)
+            copy_out_large(ot, ot % 2 == 0)
+            if ot != 1:
+                store(max(ot - 1, 0), ot, L_FIRST, C_IN, res_large[min(ot, 1)][:])

import concourse.mybir as mybir
from concourse.masks import make_identity

F32 = mybir.dt.float32
BF16 = mybir.dt.bfloat16
U32 = mybir.dt.uint32
U8 = mybir.dt.uint8
FP8X4 = mybir.dt.float8_e4m3fn_x4

P = 128
N_IMG, C_IN, C_OUT, H, W, KH, KW = 2, 128, 384, 18, 18, 3, 3
HO, WO = H - KH + 1, W - KW + 1
TAPS = KH * KW
W_WORDS = W // 2
WO_WORDS = WO // 2
ROW_PAIRS = HO // 2
ROW_SETS = KH + 1
O_TILES = C_OUT // P
BANK = 512
PSUM_BANKS = 8
C_S = 40
S_GROUPS = (0, C_S)
SLICE = 128
C_L = C_IN - 2 * C_S
L_FIRST = 2 * C_S
L_COLS = 512
KW_ORDER = (0, 2, 1)
IDLE_MATMULS_HEAD = 4

FLOPS = 2 * C_OUT * C_IN * TAPS * N_IMG * HO * WO


def tile_model_pa_s_kernel(tc, x, grad_output, out):
    nc = tc.nc

    with tc.tile_pool(name="keep", bufs=1) as keep, tc.psum_pool(name="psum", bufs=PSUM_BANKS - KW) as psum, tc.manual_schedule():

        def copy(on_scalar, dst, src):
            if on_scalar:
                nc.scalar.copy(out=dst, in_=src)
            else:
                nc.vector.tensor_copy(out=dst, in_=src)

        zeros = keep.tile([P, P], F32)
        nc.vector.memset(zeros[:], 0.0)

        def multiply_zeros(matmuls):
            idle_acc = psum.tile([P, P], F32, tag="bank", name="idle_acc")
            for i in range(matmuls):
                nc.tensor.matmul(out=idle_acc[:], lhsT=zeros[:], rhs=zeros[:], start=True, stop=True)

        x_rows = x.rearrange("n c h w -> c n (h w)")
        x_even = keep.tile([P, N_IMG, H * W], BF16)
        g_in = [keep.tile([P, N_IMG * HO * WO], BF16, name="g_in%d" % ot) for ot in range(O_TILES)]

        def load_grad(ot):
            nc.sync.dma_start(
                out=g_in[ot][:].rearrange("o (n k) -> o n k", n=N_IMG),
                in_=grad_output[:, ot * P : (ot + 1) * P].rearrange("n o i j -> o n (i j)"),
            )

        nc.sync.dma_start(out=x_even[:], in_=x_rows)
        load_grad(0)
        load_grad(1)
        load_grad(2)

        ident = keep.tile([P, P], F32)
        make_identity(nc, ident[:])

        s_grouped, s_codes, s_scales = [], [], []
        for grp in range(len(S_GROUPS)):
            grouped = keep.tile([P, KW, 4 * SLICE], BF16, align_bytes=64, name="s_grouped%d" % grp)
            nc.vector.memset(grouped[:, :, 4 * KH * C_S :], 0.0)
            s_grouped.append(grouped)
            s_codes.append(keep.tile([P, KW * SLICE], U32, align_bytes=64, name="s_codes%d" % grp))
            s_scales.append(keep.tile([P, KW * SLICE], U8, align_bytes=64, name="s_scales%d" % grp))
        l_grouped = keep.tile([P, 4 * L_COLS], BF16, align_bytes=64)
        l_codes = keep.tile([P, L_COLS], U32, align_bytes=64)
        l_scales = keep.tile([P, L_COLS], U8, align_bytes=64)
        nc.vector.memset(l_grouped[:, 4 * TAPS * C_L :], 0.0)
        g_grouped = [
            keep.tile([P, 4 * P], BF16, align_bytes=64, name="g_grouped%d" % ot) for ot in range(O_TILES)
        ]
        g_codes = keep.tile([P, C_OUT], U32, align_bytes=64)
        g_scales = keep.tile([P, C_OUT], U8, align_bytes=64)

        x_rows_by_parity = [
            keep.tile([P, 2, H // 2, N_IMG, WO_WORDS], F32, name="x_rows_by_parity%d" % kw)
            for kw in range(KW)
        ]
        x_t = [
            psum.tile([P, ROW_SETS, P], F32, name="x_t%d" % kw, tag="x_t%d" % kw, bufs=1)
            for kw in range(KW)
        ]

        def gather_window_rows(kw):
            if kw % 2:
                nc.scalar.copy(
                    out=x_rows_by_parity[kw][:].bitcast(BF16),
                    in_=x_even[:].rearrange("c n (h w) -> c n h w", w=W)[:, :, :, kw : kw + WO].rearrange(
                        "c n (m b) w -> c b m n w", b=2
                    ),
                )
                return
            words = x_even[:].bitcast(F32).rearrange("c n (h w) -> c n h w", w=W_WORDS)
            nc.vector.tensor_copy(
                out=x_rows_by_parity[kw][:],
                in_=words[:, :, :, kw // 2 : kw // 2 + WO_WORDS].rearrange("c n (m b) w -> c b m n w", b=2),
            )

        def transpose_window_rows(kw):
            for r in range(ROW_SETS):
                row_set = x_rows_by_parity[kw][:, r % 2, r // 2 : r // 2 + ROW_PAIRS, :, :]
                nc.tensor.transpose(
                    out=x_t[kw][:, r, :], in_=row_set.rearrange("c m n w -> c (m n w)"), identity=ident[:]
                )

        def group_words(dst, kw, first_c, channels, on_scalar):
            words = dst.bitcast(F32)[:, 0 : 2 * KH * channels].rearrange("p (kh c u) -> p kh c u", kh=KH, u=2)
            rows = x_t[kw][:, :, first_c : first_c + channels]
            copy(on_scalar, words[:, 0:KH:2, :, :], rows.rearrange("p (a u) c -> p a c u", u=2))
            copy(on_scalar, words[:, 1, :, :], rows[:, 1:3, :].rearrange("p u c -> p c u"))

        def group_small(grp, kw, on_scalar):
            group_words(s_grouped[grp][:, kw, :], kw, S_GROUPS[grp], C_S, on_scalar)

        def group_large(kw, on_scalar):
            width = 4 * KH * C_L
            group_words(l_grouped[:, kw * width : (kw + 1) * width], kw, L_FIRST, C_L, on_scalar)

        def quantise_small(grp, kw):
            cols = slice(kw * SLICE, (kw + 1) * SLICE)
            nc.vector.quantize_mx(
                out=s_codes[grp][:, cols].bitcast(FP8X4),
                scales=s_scales[grp][:, cols],
                in_=s_grouped[grp][:, kw, :],
            )

        def quantise_large(lo, hi):
            nc.vector.quantize_mx(
                out=l_codes[:, lo:hi].bitcast(FP8X4), scales=l_scales[:, lo:hi], in_=l_grouped[:, 4 * lo : 4 * hi]
            )

        g_row_sets = [keep.tile([P, 2, P], F32, name="g_row_sets%d" % ot) for ot in range(O_TILES)]
        g_t = {}

        def split_grad_rows(ot, on_scalar):
            copy(
                on_scalar,
                g_row_sets[ot][:].rearrange("o u (m n w) -> o u m n w", n=N_IMG, w=WO_WORDS),
                g_in[ot][:].bitcast(F32).rearrange("o (n m u w) -> o u m n w", n=N_IMG, u=2, w=WO_WORDS),
            )

        def transpose_grad_rows(ot):
            g_t[ot] = psum.tile([P, 2, P], F32, tag="bank", name="g_t%d" % ot)
            for u in range(2):
                nc.tensor.transpose(out=g_t[ot][:, u, :], in_=g_row_sets[ot][:, u, :], identity=ident[:])

        def group_grad_words(ot, on_scalar):
            copy(
                on_scalar,
                g_grouped[ot][:].bitcast(F32).rearrange("p (o u) -> p o u", u=2),
                g_t[ot][:].rearrange("p u o -> p o u"),
            )

        def quantise_grad(ot):
            o_cols = slice(ot * P, (ot + 1) * P)
            nc.vector.quantize_mx(
                out=g_codes[:, o_cols].bitcast(FP8X4), scales=g_scales[:, o_cols], in_=g_grouped[ot][:]
            )

        def one_pass(ot, acc, codes, scales):
            o_cols = slice(ot * P, (ot + 1) * P)
            nc.tensor.matmul_mx(
                out=acc,
                lhsT=g_codes[:, o_cols].bitcast(FP8X4),
                lhsT_scale=g_scales[:, o_cols],
                rhs=codes.bitcast(FP8X4),
                rhs_scale=scales,
                start=True,
                stop=True,
            )

        accs = {}

        def multiply_small(grp, ot):
            accs[(grp, ot)] = psum.tile([P, KW, SLICE], F32, tag="bank", name="acc_small")
            for kw in KW_ORDER:
                cols = slice(kw * SLICE, (kw + 1) * SLICE)
                one_pass(ot, accs[(grp, ot)][:, kw, :], s_codes[grp][:, cols], s_scales[grp][:, cols])

        def multiply_large(ot):
            accs[("large", ot)] = psum.tile([P, L_COLS], F32, tag="bank", name="acc_large")
            one_pass(ot, accs[("large", ot)][:], l_codes[:], l_scales[:])

        res_small = [keep.tile([P, n, TAPS * L_FIRST], F32, name="res_small%d" % n) for n in (1, O_TILES - 1)]
        res_large = [keep.tile([P, n, TAPS * C_L], F32, name="res_large%d" % n) for n in (1, O_TILES - 1)]

        def store(first_ot, last_ot, first_c, end_c, res):
            nc.sync.dma_start(
                out=out[first_ot * P : (last_ot + 1) * P, first_c:end_c].rearrange(
                    "(s o) c kh kw -> o s (c kh kw)", o=P
                ),
                in_=res,
            )

        def copy_out_small(grp, ot, on_scalar):
            first = TAPS * S_GROUPS[grp]
            copy(
                on_scalar,
                res_small[min(ot, 1)][:, max(ot - 1, 0), first : first + TAPS * C_S].rearrange(
                    "o (c kh kw) -> o c kh kw", kh=KH, kw=KW
                ),
                accs[(grp, ot)][:, :, 0 : KH * C_S].rearrange("o kw (kh c) -> o c kh kw", kh=KH),
            )

        def store_small(grp, first_ot, last_ot):
            first_c, end_c = S_GROUPS[grp], S_GROUPS[grp] + C_S
            s = slice(max(first_ot - 1, 0), max(last_ot - 1, 0) + 1)
            store(first_ot, last_ot, first_c, end_c, res_small[min(first_ot, 1)][:, s, TAPS * first_c : TAPS * end_c])

        def copy_out_large(ot, on_scalar):
            copy(
                on_scalar,
                res_large[min(ot, 1)][:, max(ot - 1, 0), :].rearrange("o (c kh kw) -> o c kh kw", kh=KH, kw=KW),
                accs[("large", ot)][:, 0 : TAPS * C_L].rearrange("o (kw kh c) -> o c kh kw", kh=KH, kw=KW),
            )

        SC, VE = True, False
        half = L_COLS // 2
        multiply_zeros(IDLE_MATMULS_HEAD)
        gather_window_rows(0)
        gather_window_rows(1)
        transpose_window_rows(0)
        gather_window_rows(2)
        split_grad_rows(0, VE)
        transpose_grad_rows(0)
        transpose_window_rows(2)
        transpose_window_rows(1)
        split_grad_rows(1, VE)
        split_grad_rows(2, VE)
        transpose_grad_rows(1)
        transpose_grad_rows(2)
        group_small(0, 0, SC)
        group_grad_words(0, VE)
        group_small(1, 0, SC)
        group_small(0, 2, SC)
        group_small(1, 2, SC)
        quantise_small(0, 0)
        quantise_grad(0)
        group_small(0, 1, VE)
        quantise_small(0, 2)
        quantise_small(0, 1)
        multiply_small(0, 0)
        group_grad_words(1, SC)
        group_grad_words(2, SC)
        quantise_grad(1)
        multiply_small(0, 1)
        group_small(1, 1, SC)
        group_large(1, SC)
        quantise_small(1, 0)
        quantise_grad(2)
        multiply_small(0, 2)
        quantise_small(1, 2)
        quantise_small(1, 1)
        for ot in range(O_TILES):
            copy_out_small(0, ot, SC)
            store_small(0, ot, ot)
        multiply_small(1, 0)
        group_large(2, VE)
        group_large(0, VE)
        quantise_large(half, L_COLS)
        quantise_large(0, half)
        copy_out_small(1, 0, SC)
        store_small(1, 0, 0)
        multiply_small(1, 1)
        copy_out_small(1, 1, SC)
        multiply_small(1, 2)
        copy_out_small(1, 2, VE)
        store_small(1, 1, 2)
        for ot in range(O_TILES):
            multiply_large(ot)
            copy_out_large(ot, ot % 2 == 0)
            if ot != 1:
                store(max(ot - 1, 0), ot, L_FIRST, C_IN, res_large[min(ot, 1)][:])
